import numpy as np
import ml_dtypes


def mxq(x, axis, fmt="e4m3"):
    dtype, down = {"e4m3": (ml_dtypes.float8_e4m3fn, 7), "e5m2": (ml_dtypes.float8_e5m2, 14)}[fmt]
    v = np.moveaxis(np.asarray(x, np.float32).astype(ml_dtypes.bfloat16).astype(np.float64), axis, -1)
    blocks = v.reshape(v.shape[:-1] + (-1, 32))
    amax = np.abs(blocks).max(-1, keepdims=True)
    byte = np.maximum(np.where(amax > 0, np.frexp(amax)[1] - 1 + 127, 0) - down, 1)
    scale = np.exp2(byte - 127.0)
    codes = (blocks / scale).astype(np.float32).astype(dtype).astype(np.float64)
    return np.moveaxis((codes * scale).reshape(v.shape), -1, axis)


WIDE = False


def mx_kscale(k):
    if not WIDE:
        return np.ones(k)
    levels = np.array([10, -10, 5, -5, 0])
    a = np.random.permutation(np.resize(levels, k // 512 * 4)).reshape(k // 512, 4)
    idx = np.arange(k)
    return np.exp2(a[idx // 512, idx % 128 // 32])


BF16 = ml_dtypes.bfloat16


def bf(x):
    return np.asarray(x, np.float32).astype(BF16)


def f64(x):
    return np.asarray(x).astype(np.float64)


B, L, S, D, H = 2, 384, 128, 1024, 8
HD = D // H
T = S + L


def to_mha(t):
    return t.reshape(t.shape[0], t.shape[1], H, HD).transpose(0, 2, 1, 3)


def setup_inputs():
    s = mx_kscale(D)
    return {
        "q_rot": bf(np.random.standard_normal((B, H, T, HD))),
        "k_rot": bf(np.random.standard_normal((B, H, T, HD))),
        "x": bf(np.random.standard_normal((B, L, D)) * s),
        "c": bf(np.random.standard_normal((B, S, D)) * s),
        "Wv_x": bf(np.random.standard_normal((D, D)) * 3.0 / np.sqrt(D) / s[:, None]),
        "bv_x": bf(np.random.standard_normal(D) * 0.2),
        "Wv_c": bf(np.random.standard_normal((D, D)) * 3.0 / np.sqrt(D) / s[:, None]),
        "bv_c": bf(np.random.standard_normal(D) * 0.2),
    }


def reference(q_rot, k_rot, x, c, Wv_x, bv_x, Wv_c, bv_c):
    vc = to_mha((mxq(f64(c), 2, "e4m3") @ mxq(f64(Wv_c), 0, "e4m3")) + f64(bv_c))
    vx = to_mha((mxq(f64(x), 2, "e4m3") @ mxq(f64(Wv_x), 0, "e4m3")) + f64(bv_x))
    v = np.concatenate([vc, vx], axis=2)
    scores = f64(q_rot) @ f64(k_rot).transpose(0, 1, 3, 2) / np.sqrt(HD)
    e = np.exp(scores - scores.max(-1, keepdims=True))
    y = (mxq(e, 3, "e4m3") @ mxq(v, 2, "e4m3")) / e.sum(-1, keepdims=True)
    y = y.transpose(0, 2, 1, 3).reshape(B, T, D)
    return y[:, S:], y[:, :S]

@@ -1,0 +1,269 @@
+from contextlib import ExitStack
+import math
+
+import concourse.mybir as mybir
+from concourse.masks import make_identity
+
+F32 = mybir.dt.float32
+BF16 = mybir.dt.bfloat16
+U32 = mybir.dt.uint32
+U8 = mybir.dt.uint8
+FP8X4 = mybir.dt.float8_e4m3fn_x4
+ALU = mybir.AluOpType
+ACT = mybir.ActivationFunctionType
+
+P = 128
+PACK = 4
+BATCH = 2
+HEADS = 8
+HD = 128
+D = HEADS * HD
+SEQ = 512
+TILES = SEQ // P
+PASSES = D // (P * PACK)
+ROUNDS = BATCH * HEADS
+LAG = 2
+SCALE = 1.0 / math.sqrt(HD)
+
+FLOPS = 2 * BATCH * SEQ * D * D + 2 * 2 * ROUNDS * SEQ * SEQ * HD
+
+
+def tile_dualstreamattentionwithrotaryembedding_pb_kernel(
+    tc, q_rot, k_rot, x, c, Wv_x, bv_x, Wv_c, bv_c, out_0, out_1
+):
+    nc = tc.nc
+    with ExitStack() as ctx:
+        const = ctx.enter_context(tc.tile_pool(name="const", bufs=1))
+        raw = ctx.enter_context(tc.tile_pool(name="raw", bufs=1))
+        keep = ctx.enter_context(tc.tile_pool(name="keep", bufs=1))
+        stage = ctx.enter_context(tc.tile_pool(name="stage", bufs=2))
+        epool = ctx.enter_context(tc.tile_pool(name="epool", bufs=4))
+        ecodes = ctx.enter_context(tc.tile_pool(name="ecodes", bufs=6))
+        small = ctx.enter_context(tc.tile_pool(name="small", bufs=8))
+        ps_scores = ctx.enter_context(tc.psum_pool(name="ps_scores", bufs=3))
+        ps_et = ctx.enter_context(tc.psum_pool(name="ps_et", bufs=2))
+        ps_in = ctx.enter_context(tc.psum_pool(name="ps_in", bufs=1))
+        ps_mx = ctx.enter_context(tc.psum_pool(name="ps_mx", bufs=2))
+
+        q_raw = []
+        k_raw = []
+        for r in range(ROUNDS):
+            q_raw.append(raw.tile([P, TILES, HD], BF16, name="q_raw%d" % r))
+            k_raw.append(raw.tile([P, TILES, HD], BF16, name="k_raw%d" % r))
+        tok_raw = [raw.tile([P, TILES, D], BF16, name="tok_raw%d" % b) for b in range(BATCH)]
+        w_raw = [
+            [raw.tile([P, PASSES, PACK, HD], BF16, name="w_raw%d_%d" % (h, w)) for w in range(2)]
+            for h in range(HEADS)
+        ]
+        bias_x = const.tile([P, D], BF16)
+        bias = const.tile([P, TILES, D], BF16)
+
+        def load_qk(r):
+            h, b = divmod(r, BATCH)
+            nc.sync.dma_start(out=q_raw[r][:], in_=q_rot[b, h].rearrange("(j p) d -> p j d", p=P))
+            nc.sync.dma_start(out=k_raw[r][:], in_=k_rot[b, h].rearrange("(j p) d -> p j d", p=P))
+
+        def load_tokens(b):
+            nc.sync.dma_start(out=tok_raw[b][:, 0, :], in_=c[b])
+            nc.sync.dma_start(
+                out=tok_raw[b][:, 1:TILES, :], in_=x[b].rearrange("(j p) k -> p j k", p=P)
+            )
+
+        def load_weights(h):
+            for w, weights in enumerate((Wv_c, Wv_x)):
+                rows = weights.rearrange("(a p e) n -> p a e n", p=P, e=2)
+                slots = w_raw[h][w][:].rearrange("p g (u e) n -> p (g u) e n", e=2)
+                for e in range(2):
+                    nc.sync.dma_start(out=slots[:, :, e, :], in_=rows[:, :, e, h * HD : (h + 1) * HD])
+
+        nc.scalar.dma_start(out=bias[:, 0, :], in_=bv_c.partition_broadcast(P))
+        nc.scalar.dma_start(out=bias_x[:], in_=bv_x.partition_broadcast(P))
+        load_qk(0)
+        load_tokens(0)
+        load_weights(0)
+        load_qk(1)
+        load_tokens(1)
+        for r in range(2, ROUNDS):
+            if r % BATCH == 0:
+                load_weights(r // BATCH)
+            load_qk(r)
+
+        ident_bf = const.tile([P, P], BF16)
+        make_identity(nc, ident_bf[:])
+        ident_f32 = const.tile([P, P], F32)
+        make_identity(nc, ident_f32[:])
+
+        tok_codes = [keep.tile([P, TILES * PASSES * P], U32, name="tok_codes%d" % b, align_bytes=64) for b in range(BATCH)]
+        tok_scales = [keep.tile([P, TILES * PASSES * P], U8, name="tok_scales%d" % b, align_bytes=64) for b in range(BATCH)]
+        w_codes = [keep.tile([P, 2 * PASSES * HD], U32, name="w_codes%d" % h, align_bytes=64) for h in range(HEADS)]
+        w_scales = [keep.tile([P, 2 * PASSES * HD], U8, name="w_scales%d" % h, align_bytes=64) for h in range(HEADS)]
+        v_codes = [keep.tile([P, HD], U32, name="v_codes%d" % r, align_bytes=64) for r in range(ROUNDS)]
+        v_scales = [keep.tile([P, HD], U8, name="v_scales%d" % r, align_bytes=64) for r in range(ROUNDS)]
+
+        qk_t = {}
+        e_tiles = {}
+        e_grouped = {}
+        e_words = {}
+        row_sums = {}
+
+        def prepare_tokens(b):
+            grouped = stage.tile([P, TILES * PASSES * P * PACK], BF16, name="tok_grouped", align_bytes=64)
+            for t in range(TILES):
+                words = tok_raw[b][:, t, :].bitcast(F32)
+                flipped = ps_in.tile([P, PASSES * 2, P], F32, name="flipped", tag="ps_in")
+                for a in range(PASSES * 2):
+                    nc.tensor.transpose(flipped[:, a, :], words[:, a * P : (a + 1) * P], ident_f32[:])
+                span = PASSES * P * PACK
+                nc.scalar.copy(
+                    out=grouped[:, t * span : (t + 1) * span]
+                    .bitcast(F32)
+                    .rearrange("p (g m u) -> p g m u", g=PASSES, u=2),
+                    in_=flipped[:].rearrange("p (g u) m -> p g m u", u=2),
+                )
+            nc.vector.quantize_mx(
+                out=tok_codes[b][:].bitcast(FP8X4), scales=tok_scales[b][:], in_=grouped[:]
+            )
+
+        def transpose_qk(r):
+            flipped = ps_in.tile([P, 2 * SEQ], BF16, name="qk_flipped", tag="ps_in")
+            for j in range(TILES):
+                nc.tensor.transpose(flipped[:, j * P : (j + 1) * P], q_raw[r][:, j, :], ident_bf[:])
+            for j in range(TILES):
+                nc.tensor.transpose(
+                    flipped[:, SEQ + j * P : SEQ + (j + 1) * P], k_raw[r][:, j, :], ident_bf[:]
+                )
+            qk_t[r] = stage.tile([P, 2 * SEQ], BF16, name="qk_t", bufs=3)
+            nc.vector.tensor_copy(out=qk_t[r][:], in_=flipped[:])
+
+        def softmax_tile(r, j):
+            if j == 0:
+                row_sums[r] = small.tile([P, TILES], F32, name="row_sums")
+            scores = ps_scores.tile([P, SEQ], F32, name="scores")
+            nc.tensor.matmul(
+                out=scores[:],
+                lhsT=qk_t[r][:, j * P : (j + 1) * P],
+                rhs=qk_t[r][:, SEQ : 2 * SEQ],
+                start=True,
+                stop=True,
+            )
+            row_max = small.tile([P, 1], F32, name="row_max")
+            nc.vector.tensor_reduce(out=row_max[:], in_=scores[:], axis=mybir.AxisListType.X, op=ALU.max)
+            shift = small.tile([P, 1], F32, name="shift")
+            nc.vector.tensor_scalar_mul(out=shift[:], in0=row_max[:], scalar1=-SCALE)
+            e = epool.tile([P, SEQ], BF16, name="e")
+            nc.scalar.activation(
+                out=e[:],
+                in_=scores[:],
+                func=ACT.Exp,
+                bias=shift[:],
+                scale=SCALE,
+                accum_out=row_sums[r][:, j : j + 1],
+            )
+            e_tiles[(r, j)] = e
+
+        def transpose_e(r, j):
+            if j == 0:
+                e_grouped[r] = stage.tile([P, SEQ * PACK], BF16, name="e_grouped", align_bytes=64)
+            e = e_tiles[(r, j)]
+            flipped = ps_et.tile([P, TILES, P], BF16, name="e_flipped")
+            for t in range(TILES):
+                nc.tensor.transpose(flipped[:, t, :], e[:, t * P : (t + 1) * P], ident_bf[:])
+            span = P * PACK
+            nc.scalar.copy(
+                out=e_grouped[r][:, j * span : (j + 1) * span].rearrange("p (m t) -> p m t", t=PACK),
+                in_=flipped[:].rearrange("p t m -> p m t"),
+            )
+            if j == TILES - 1:
+                codes = ecodes.tile([P, SEQ], U32, name="e_codes", align_bytes=64)
+                scales = ecodes.tile([P, SEQ], U8, name="e_scales", align_bytes=64)
+                nc.vector.quantize_mx(out=codes[:].bitcast(FP8X4), scales=scales[:], in_=e_grouped[r][:])
+                e_words[r] = (codes, scales)
+
+        def prepare_weights(h):
+            grouped = stage.tile([P, 2 * PASSES * HD * PACK], BF16, name="w_grouped", align_bytes=64)
+            span = PASSES * HD * PACK
+            for w in range(2):
+                nc.vector.tensor_copy(
+                    out=grouped[:, w * span : (w + 1) * span].rearrange(
+                        "p (g n t) -> p g n t", g=PASSES, t=PACK
+                    ),
+                    in_=w_raw[h][w][:].rearrange("p g t n -> p g n t"),
+                )
+            nc.vector.quantize_mx(out=w_codes[h][:].bitcast(FP8X4), scales=w_scales[h][:], in_=grouped[:])
+
+        def project_values(r):
+            h, b = divmod(r, BATCH)
+            acc = ps_mx.tile([P, TILES, HD], F32, name="v_acc", tag="ps_mx")
+            for t in range(TILES):
+                w = 0 if t == 0 else 1
+                for g in range(PASSES):
+                    tok = slice((t * PASSES + g) * P, (t * PASSES + g + 1) * P)
+                    col = slice((w * PASSES + g) * HD, (w * PASSES + g + 1) * HD)
+                    nc.tensor.matmul_mx(
+                        out=acc[:, t, :],
+                        lhsT=tok_codes[b][:, tok].bitcast(FP8X4),
+                        lhsT_scale=tok_scales[b][:, tok],
+                        rhs=w_codes[h][:, col].bitcast(FP8X4),
+                        rhs_scale=w_scales[h][:, col],
+                        start=(g == 0),
+                        stop=(g == PASSES - 1),
+                    )
+            grouped = stage.tile([P, HD * PACK], BF16, name="v_grouped", align_bytes=64)
+            nc.vector.tensor_tensor(
+                out=grouped[:].rearrange("p (n t) -> p n t", t=PACK),
+                in0=acc[:].rearrange("p t n -> p n t"),
+                in1=bias[:, :, h * HD : (h + 1) * HD].rearrange("p t n -> p n t"),
+                op=ALU.add,
+            )
+            nc.vector.quantize_mx(out=v_codes[r][:].bitcast(FP8X4), scales=v_scales[r][:], in_=grouped[:])
+
+        def attend(r):
+            h, b = divmod(r, BATCH)
+            codes, scales = e_words[r]
+            acc = ps_mx.tile([P, TILES, HD], F32, name="y_acc", tag="ps_mx")
+            for j in range(TILES):
+                nc.tensor.matmul_mx(
+                    out=acc[:, j, :],
+                    lhsT=codes[:, j * P : (j + 1) * P].bitcast(FP8X4),
+                    lhsT_scale=scales[:, j * P : (j + 1) * P],
+                    rhs=v_codes[r][:].bitcast(FP8X4),
+                    rhs_scale=v_scales[r][:],
+                    start=True,
+                    stop=True,
+                )
+            inv = small.tile([P, TILES], F32, name="inv")
+            nc.vector.reciprocal(out=inv[:], in_=row_sums[r][:])
+            y = stage.tile([P, TILES, HD], F32, name="y", bufs=3)
+            nc.vector.tensor_tensor(
+                out=y[:], in0=acc[:], in1=inv[:].unsqueeze(2).to_broadcast([P, TILES, HD]), op=ALU.mult
+            )
+            cols = slice(h * HD, (h + 1) * HD)
+            nc.sync.dma_start(out=out_1[b, :, cols], in_=y[:, 0, :])
+            nc.sync.dma_start(
+                out=out_0[b].rearrange("(j p) d -> p j d", p=P)[:, :, cols], in_=y[:, 1:TILES, :]
+            )
+
+        def spread_bias():
+            nc.vector.tensor_copy(
+                out=bias[:, 1:TILES, :], in_=bias_x[:].unsqueeze(1).to_broadcast([P, TILES - 1, D])
+            )
+
+        transpose_qk(0)
+        for n in range((ROUNDS + 1) * TILES):
+            r, j = divmod(n, TILES)
+            if j == 0 and r + 1 < ROUNDS:
+                transpose_qk(r + 1)
+            if j == 1 and r >= 1:
+                project_values(r - 1)
+            if r < ROUNDS:
+                softmax_tile(r, j)
+            if LAG <= n < ROUNDS * TILES + LAG:
+                transpose_e((n - LAG) // TILES, (n - LAG) % TILES)
+            if j == 2 and r < BATCH:
+                prepare_tokens(r)
+            if j == 3 and r == 0:
+                spread_bias()
+            if j == 3 and r >= 1:
+                attend(r - 1)
+            if j == 3 and r % BATCH == 0 and r < ROUNDS:
+                prepare_weights(r // BATCH)

@@ -22,7 +22,6 @@ SEQ = 512
 TILES = SEQ // P
 PASSES = D // (P * PACK)
 ROUNDS = BATCH * HEADS
-LAG = 2
 SCALE = 1.0 / math.sqrt(HD)
 
 FLOPS = 2 * BATCH * SEQ * D * D + 2 * 2 * ROUNDS * SEQ * SEQ * HD
@@ -37,13 +36,10 @@ def tile_dualstreamattentionwithrotaryembedding_pb_kernel(
         raw = ctx.enter_context(tc.tile_pool(name="raw", bufs=1))
         keep = ctx.enter_context(tc.tile_pool(name="keep", bufs=1))
         stage = ctx.enter_context(tc.tile_pool(name="stage", bufs=2))
-        epool = ctx.enter_context(tc.tile_pool(name="epool", bufs=4))
-        ecodes = ctx.enter_context(tc.tile_pool(name="ecodes", bufs=6))
         small = ctx.enter_context(tc.tile_pool(name="small", bufs=8))
-        ps_scores = ctx.enter_context(tc.psum_pool(name="ps_scores", bufs=3))
+        ps_scores = ctx.enter_context(tc.psum_pool(name="ps_scores", bufs=4))
         ps_et = ctx.enter_context(tc.psum_pool(name="ps_et", bufs=2))
-        ps_in = ctx.enter_context(tc.psum_pool(name="ps_in", bufs=1))
-        ps_mx = ctx.enter_context(tc.psum_pool(name="ps_mx", bufs=2))
+        ps_misc = ctx.enter_context(tc.psum_pool(name="ps_misc", bufs=2))
 
         q_raw = []
         k_raw = []
@@ -51,10 +47,7 @@ def tile_dualstreamattentionwithrotaryembedding_pb_kernel(
             q_raw.append(raw.tile([P, TILES, HD], BF16, name="q_raw%d" % r))
             k_raw.append(raw.tile([P, TILES, HD], BF16, name="k_raw%d" % r))
         tok_raw = [raw.tile([P, TILES, D], BF16, name="tok_raw%d" % b) for b in range(BATCH)]
-        w_raw = [
-            [raw.tile([P, PASSES, PACK, HD], BF16, name="w_raw%d_%d" % (h, w)) for w in range(2)]
-            for h in range(HEADS)
-        ]
+        w_raw = [raw.tile([P, PASSES, PACK, HD], BF16, name="w_raw%d" % i) for i in range(2 * HEADS)]
         bias_x = const.tile([P, D], BF16)
         bias = const.tile([P, TILES, D], BF16)
 
@@ -72,19 +65,20 @@ def tile_dualstreamattentionwithrotaryembedding_pb_kernel(
         def load_weights(h):
             for w, weights in enumerate((Wv_c, Wv_x)):
                 rows = weights.rearrange("(a p e) n -> p a e n", p=P, e=2)
-                slots = w_raw[h][w][:].rearrange("p g (u e) n -> p (g u) e n", e=2)
+                slots = w_raw[2 * h + w][:].rearrange("p g (u e) n -> p (g u) e n", e=2)
                 for e in range(2):
                     nc.sync.dma_start(out=slots[:, :, e, :], in_=rows[:, :, e, h * HD : (h + 1) * HD])
 
         nc.scalar.dma_start(out=bias[:, 0, :], in_=bv_c.partition_broadcast(P))
         nc.scalar.dma_start(out=bias_x[:], in_=bv_x.partition_broadcast(P))
         load_qk(0)
+        load_qk(1)
         load_tokens(0)
         load_weights(0)
-        load_qk(1)
+        load_qk(2)
         load_tokens(1)
-        for r in range(2, ROUNDS):
-            if r % BATCH == 0:
+        for r in range(3, ROUNDS):
+            if r % BATCH == 1:
                 load_weights(r // BATCH)
             load_qk(r)
 
@@ -95,45 +89,61 @@ def tile_dualstreamattentionwithrotaryembedding_pb_kernel(
 
         tok_codes = [keep.tile([P, TILES * PASSES * P], U32, name="tok_codes%d" % b, align_bytes=64) for b in range(BATCH)]
         tok_scales = [keep.tile([P, TILES * PASSES * P], U8, name="tok_scales%d" % b, align_bytes=64) for b in range(BATCH)]
-        w_codes = [keep.tile([P, 2 * PASSES * HD], U32, name="w_codes%d" % h, align_bytes=64) for h in range(HEADS)]
-        w_scales = [keep.tile([P, 2 * PASSES * HD], U8, name="w_scales%d" % h, align_bytes=64) for h in range(HEADS)]
-        v_codes = [keep.tile([P, HD], U32, name="v_codes%d" % r, align_bytes=64) for r in range(ROUNDS)]
-        v_scales = [keep.tile([P, HD], U8, name="v_scales%d" % r, align_bytes=64) for r in range(ROUNDS)]
+        w_codes = [keep.tile([P, PASSES * HD], U32, name="w_codes%d" % i, align_bytes=64) for i in range(2 * HEADS)]
+        w_scales = [keep.tile([P, PASSES * HD], U8, name="w_scales%d" % i, align_bytes=64) for i in range(2 * HEADS)]
 
+        tok_grouped = {}
         qk_t = {}
         e_tiles = {}
+        e_flipped = {}
+        w_grouped = {}
         e_grouped = {}
         e_words = {}
+        v_words = {}
+        v_acc = {}
+        y_acc = {}
         row_sums = {}
 
-        def prepare_tokens(b):
-            grouped = stage.tile([P, TILES * PASSES * P * PACK], BF16, name="tok_grouped", align_bytes=64)
+        def transpose_tokens(b):
+            tok_grouped[b] = stage.tile([P, TILES * PASSES * P * PACK], BF16, name="tok_grouped", align_bytes=64)
             for t in range(TILES):
                 words = tok_raw[b][:, t, :].bitcast(F32)
-                flipped = ps_in.tile([P, PASSES * 2, P], F32, name="flipped", tag="ps_in")
+                flipped = ps_misc.tile([P, PASSES * 2, P], F32, name="tok_flipped", tag="misc")
                 for a in range(PASSES * 2):
                     nc.tensor.transpose(flipped[:, a, :], words[:, a * P : (a + 1) * P], ident_f32[:])
                 span = PASSES * P * PACK
                 nc.scalar.copy(
-                    out=grouped[:, t * span : (t + 1) * span]
+                    out=tok_grouped[b][:, t * span : (t + 1) * span]
                     .bitcast(F32)
                     .rearrange("p (g m u) -> p g m u", g=PASSES, u=2),
                     in_=flipped[:].rearrange("p (g u) m -> p g m u", u=2),
                 )
+
+        def quantise_tokens(b):
             nc.vector.quantize_mx(
-                out=tok_codes[b][:].bitcast(FP8X4), scales=tok_scales[b][:], in_=grouped[:]
+                out=tok_codes[b][:].bitcast(FP8X4), scales=tok_scales[b][:], in_=tok_grouped[b][:]
             )
 
+        def spread_bias():
+            nc.vector.tensor_copy(
+                out=bias[:, 1:TILES, :], in_=bias_x[:].unsqueeze(1).to_broadcast([P, TILES - 1, D])
+            )
+
+        qk_flipped = {}
+
         def transpose_qk(r):
-            flipped = ps_in.tile([P, 2 * SEQ], BF16, name="qk_flipped", tag="ps_in")
+            flipped = ps_misc.tile([P, 2 * SEQ], BF16, name="qk_flipped", tag="misc")
             for j in range(TILES):
                 nc.tensor.transpose(flipped[:, j * P : (j + 1) * P], q_raw[r][:, j, :], ident_bf[:])
             for j in range(TILES):
                 nc.tensor.transpose(
                     flipped[:, SEQ + j * P : SEQ + (j + 1) * P], k_raw[r][:, j, :], ident_bf[:]
                 )
+            qk_flipped[r] = flipped
+
+        def copy_qk(r):
             qk_t[r] = stage.tile([P, 2 * SEQ], BF16, name="qk_t", bufs=3)
-            nc.vector.tensor_copy(out=qk_t[r][:], in_=flipped[:])
+            nc.scalar.copy(out=qk_t[r][:], in_=qk_flipped[r][:])
 
         def softmax_tile(r, j):
             if j == 0:
@@ -146,11 +156,18 @@ def tile_dualstreamattentionwithrotaryembedding_pb_kernel(
                 start=True,
                 stop=True,
             )
-            row_max = small.tile([P, 1], F32, name="row_max")
-            nc.vector.tensor_reduce(out=row_max[:], in_=scores[:], axis=mybir.AxisListType.X, op=ALU.max)
             shift = small.tile([P, 1], F32, name="shift")
-            nc.vector.tensor_scalar_mul(out=shift[:], in0=row_max[:], scalar1=-SCALE)
-            e = epool.tile([P, SEQ], BF16, name="e")
+            scaled = stage.tile([P, SEQ], BF16, name="scaled")
+            nc.vector.tensor_scalar(
+                out=scaled[:],
+                in0=scores[:],
+                scalar1=-SCALE,
+                scalar2=None,
+                op0=ALU.mult,
+                op1=ALU.min,
+                accum_out=shift[:],
+            )
+            e = stage.tile([P, SEQ], BF16, name="e", bufs=6)
             nc.scalar.activation(
                 out=e[:],
                 in_=scores[:],
@@ -161,81 +178,111 @@ def tile_dualstreamattentionwithrotaryembedding_pb_kernel(
             )
             e_tiles[(r, j)] = e
 
-        def transpose_e(r, j):
-            if j == 0:
-                e_grouped[r] = stage.tile([P, SEQ * PACK], BF16, name="e_grouped", align_bytes=64)
-            e = e_tiles[(r, j)]
-            flipped = ps_et.tile([P, TILES, P], BF16, name="e_flipped")
-            for t in range(TILES):
-                nc.tensor.transpose(flipped[:, t, :], e[:, t * P : (t + 1) * P], ident_bf[:])
-            span = P * PACK
-            nc.scalar.copy(
-                out=e_grouped[r][:, j * span : (j + 1) * span].rearrange("p (m t) -> p m t", t=PACK),
-                in_=flipped[:].rearrange("p t m -> p m t"),
+        def regroup(out, in_):
+            nc.gpsimd.tensor_scalar(
+                out=out.rearrange("p (a m t) -> p a m t", m=P, t=PACK),
+                in0=in_.rearrange("p (a t m) -> p a m t", m=P, t=PACK),
+                scalar1=1.0,
+                scalar2=0.0,
+                op0=ALU.mult,
+                op1=ALU.add,
             )
-            if j == TILES - 1:
-                codes = ecodes.tile([P, SEQ], U32, name="e_codes", align_bytes=64)
-                scales = ecodes.tile([P, SEQ], U8, name="e_scales", align_bytes=64)
-                nc.vector.quantize_mx(out=codes[:].bitcast(FP8X4), scales=scales[:], in_=e_grouped[r][:])
-                e_words[r] = (codes, scales)
 
-        def prepare_weights(h):
-            grouped = stage.tile([P, 2 * PASSES * HD * PACK], BF16, name="w_grouped", align_bytes=64)
-            span = PASSES * HD * PACK
-            for w in range(2):
-                nc.vector.tensor_copy(
-                    out=grouped[:, w * span : (w + 1) * span].rearrange(
-                        "p (g n t) -> p g n t", g=PASSES, t=PACK
-                    ),
-                    in_=w_raw[h][w][:].rearrange("p g t n -> p g n t"),
+        def transpose_e(r, j):
+            if j % 2 == 0:
+                e_flipped[(r, j // 2)] = ps_et.tile([P, 2, TILES, P], BF16, name="e_flipped")
+            e = e_tiles[(r, j)]
+            for t in range(TILES):
+                nc.tensor.transpose(
+                    e_flipped[(r, j // 2)][:, j % 2, t, :], e[:, t * P : (t + 1) * P], ident_bf[:]
                 )
-            nc.vector.quantize_mx(out=w_codes[h][:].bitcast(FP8X4), scales=w_scales[h][:], in_=grouped[:])
+
+        def copy_e(r, pair):
+            if pair == 0:
+                e_grouped[r] = stage.tile([P, SEQ * PACK], BF16, name="e_grouped", align_bytes=64, bufs=3)
+            planes = stage.tile([P, 2 * TILES * P], BF16, name="e_planes", bufs=3)
+            nc.scalar.copy(out=planes[:], in_=e_flipped[(r, pair)][:].rearrange("p a t m -> p (a t m)"))
+            span = 2 * P * PACK
+            regroup(e_grouped[r][:, pair * span : (pair + 1) * span], planes[:])
+
+        def quantise_e(r):
+            codes = stage.tile([P, SEQ], U32, name="e_codes", align_bytes=64)
+            scales = stage.tile([P, SEQ], U8, name="e_scales", align_bytes=64)
+            nc.vector.quantize_mx(out=codes[:].bitcast(FP8X4), scales=scales[:], in_=e_grouped[r][:])
+            e_words[r] = (codes, scales)
+
+        def regroup_weights(i):
+            grouped = stage.tile([P, PASSES * HD * PACK], BF16, name="w_grouped", align_bytes=64)
+            if i % 2 == 0:
+                regroup(grouped[:], w_raw[i][:].rearrange("p g t n -> p (g t n)"))
+            else:
+                nc.vector.tensor_copy(
+                    out=grouped[:].rearrange("p (g n t) -> p g n t", g=PASSES, t=PACK),
+                    in_=w_raw[i][:].rearrange("p g t n -> p g n t"),
+                )
+            w_grouped[i] = grouped
+
+        def quantise_weights(i):
+            nc.vector.quantize_mx(
+                out=w_codes[i][:].bitcast(FP8X4), scales=w_scales[i][:], in_=w_grouped[i][:]
+            )
 
         def project_values(r):
             h, b = divmod(r, BATCH)
-            acc = ps_mx.tile([P, TILES, HD], F32, name="v_acc", tag="ps_mx")
+            acc = ps_misc.tile([P, TILES, HD], F32, name="v_acc", tag="misc")
             for t in range(TILES):
-                w = 0 if t == 0 else 1
+                i = 2 * h + (0 if t == 0 else 1)
                 for g in range(PASSES):
                     tok = slice((t * PASSES + g) * P, (t * PASSES + g + 1) * P)
-                    col = slice((w * PASSES + g) * HD, (w * PASSES + g + 1) * HD)
+                    col = slice(g * HD, (g + 1) * HD)
                     nc.tensor.matmul_mx(
                         out=acc[:, t, :],
                         lhsT=tok_codes[b][:, tok].bitcast(FP8X4),
                         lhsT_scale=tok_scales[b][:, tok],
-                        rhs=w_codes[h][:, col].bitcast(FP8X4),
-                        rhs_scale=w_scales[h][:, col],
+                        rhs=w_codes[i][:, col].bitcast(FP8X4),
+                        rhs_scale=w_scales[i][:, col],
                         start=(g == 0),
                         stop=(g == PASSES - 1),
                     )
+            v_acc[r] = acc
+
+        def quantise_values(r):
+            h = r // BATCH
             grouped = stage.tile([P, HD * PACK], BF16, name="v_grouped", align_bytes=64)
             nc.vector.tensor_tensor(
                 out=grouped[:].rearrange("p (n t) -> p n t", t=PACK),
-                in0=acc[:].rearrange("p t n -> p n t"),
+                in0=v_acc[r][:].rearrange("p t n -> p n t"),
                 in1=bias[:, :, h * HD : (h + 1) * HD].rearrange("p t n -> p n t"),
                 op=ALU.add,
             )
-            nc.vector.quantize_mx(out=v_codes[r][:].bitcast(FP8X4), scales=v_scales[r][:], in_=grouped[:])
+            codes = stage.tile([P, HD], U32, name="v_codes", align_bytes=64)
+            scales = stage.tile([P, HD], U8, name="v_scales", align_bytes=64)
+            nc.vector.quantize_mx(out=codes[:].bitcast(FP8X4), scales=scales[:], in_=grouped[:])
+            v_words[r] = (codes, scales)
 
         def attend(r):
-            h, b = divmod(r, BATCH)
-            codes, scales = e_words[r]
-            acc = ps_mx.tile([P, TILES, HD], F32, name="y_acc", tag="ps_mx")
+            e_codes, e_scales = e_words[r]
+            v_codes, v_scales = v_words[r]
+            acc = ps_misc.tile([P, TILES, HD], F32, name="y_acc", tag="misc")
             for j in range(TILES):
                 nc.tensor.matmul_mx(
                     out=acc[:, j, :],
-                    lhsT=codes[:, j * P : (j + 1) * P].bitcast(FP8X4),
-                    lhsT_scale=scales[:, j * P : (j + 1) * P],
-                    rhs=v_codes[r][:].bitcast(FP8X4),
-                    rhs_scale=v_scales[r][:],
+                    lhsT=e_codes[:, j * P : (j + 1) * P].bitcast(FP8X4),
+                    lhsT_scale=e_scales[:, j * P : (j + 1) * P],
+                    rhs=v_codes[:].bitcast(FP8X4),
+                    rhs_scale=v_scales[:],
                     start=True,
                     stop=True,
                 )
+            y_acc[r] = acc
+
+        def store_output(r):
+            h, b = divmod(r, BATCH)
             inv = small.tile([P, TILES], F32, name="inv")
             nc.vector.reciprocal(out=inv[:], in_=row_sums[r][:])
             y = stage.tile([P, TILES, HD], F32, name="y", bufs=3)
             nc.vector.tensor_tensor(
-                out=y[:], in0=acc[:], in1=inv[:].unsqueeze(2).to_broadcast([P, TILES, HD]), op=ALU.mult
+                out=y[:], in0=y_acc[r][:], in1=inv[:].unsqueeze(2).to_broadcast([P, TILES, HD]), op=ALU.mult
             )
             cols = slice(h * HD, (h + 1) * HD)
             nc.sync.dma_start(out=out_1[b, :, cols], in_=y[:, 0, :])
@@ -243,27 +290,58 @@ def tile_dualstreamattentionwithrotaryembedding_pb_kernel(
                 out=out_0[b].rearrange("(j p) d -> p j d", p=P)[:, :, cols], in_=y[:, 1:TILES, :]
             )
 
-        def spread_bias():
-            nc.vector.tensor_copy(
-                out=bias[:, 1:TILES, :], in_=bias_x[:].unsqueeze(1).to_broadcast([P, TILES - 1, D])
-            )
+        def round_at(step, offset):
+            r, rest = divmod(step - offset, TILES)
+            return r if rest == 0 and 0 <= r < ROUNDS else None
 
         transpose_qk(0)
-        for n in range((ROUNDS + 1) * TILES):
-            r, j = divmod(n, TILES)
-            if j == 0 and r + 1 < ROUNDS:
-                transpose_qk(r + 1)
-            if j == 1 and r >= 1:
-                project_values(r - 1)
-            if r < ROUNDS:
-                softmax_tile(r, j)
-            if LAG <= n < ROUNDS * TILES + LAG:
-                transpose_e((n - LAG) // TILES, (n - LAG) % TILES)
-            if j == 2 and r < BATCH:
-                prepare_tokens(r)
-            if j == 3 and r == 0:
+        copy_qk(0)
+        for step in range(TILES * ROUNDS + 9):
+            if step < TILES * ROUNDS:
+                softmax_tile(step // TILES, step % TILES)
+
+            r = round_at(step, 8)
+            if r is not None:
+                project_values(r)
+            r = round_at(step, 11)
+            if r is not None:
+                attend(r)
+
+            if 0 <= step - 3 < TILES * ROUNDS:
+                transpose_e((step - 3) // TILES, (step - 3) % TILES)
+            r = round_at(step, 5)
+            if r is not None:
+                copy_e(r, 0)
+            r = round_at(step, 7)
+            if r is not None:
+                copy_e(r, 1)
+            r = round_at(step, 2 - TILES)
+            if r is not None:
+                transpose_qk(r)
+            r = round_at(step, 3)
+            if r is not None and r < BATCH:
+                transpose_tokens(r)
+
+            r = round_at(step, 12)
+            if r is not None:
+                store_output(r)
+            r = round_at(step, 9)
+            if r is not None:
+                quantise_values(r)
+            r = round_at(step, 10)
+            if r is not None:
+                quantise_e(r)
+            r = round_at(step, 3 - TILES)
+            if r is not None:
+                copy_qk(r)
+            r = round_at(step, 2)
+            if r is not None:
+                regroup_weights(r)
+            r = round_at(step, 3)
+            if r is not None:
+                quantise_weights(r)
+            r = round_at(step, 4)
+            if r is not None and r < BATCH:
+                quantise_tokens(r)
+            if step == 5:
                 spread_bias()
-            if j == 3 and r >= 1:
-                attend(r - 1)
-            if j == 3 and r % BATCH == 0 and r < ROUNDS:
-                prepare_weights(r // BATCH)

@@ -37,8 +37,8 @@ def tile_dualstreamattentionwithrotaryembedding_pb_kernel(
         keep = ctx.enter_context(tc.tile_pool(name="keep", bufs=1))
         stage = ctx.enter_context(tc.tile_pool(name="stage", bufs=2))
         small = ctx.enter_context(tc.tile_pool(name="small", bufs=8))
-        ps_scores = ctx.enter_context(tc.psum_pool(name="ps_scores", bufs=4))
-        ps_et = ctx.enter_context(tc.psum_pool(name="ps_et", bufs=2))
+        ps_scores = ctx.enter_context(tc.psum_pool(name="ps_scores", bufs=3))
+        ps_et = ctx.enter_context(tc.psum_pool(name="ps_et", bufs=3))
         ps_misc = ctx.enter_context(tc.psum_pool(name="ps_misc", bufs=2))
 
         q_raw = []
@@ -94,11 +94,15 @@ def tile_dualstreamattentionwithrotaryembedding_pb_kernel(
 
         tok_grouped = {}
         qk_t = {}
-        e_tiles = {}
+        s_tiles = {}
         e_flipped = {}
+        u_tiles = {}
+        e_tiles = {}
         w_grouped = {}
         e_grouped = {}
         e_words = {}
+        v_grouped = {}
+        inverse = {}
         v_words = {}
         v_acc = {}
         y_acc = {}
@@ -143,11 +147,9 @@ def tile_dualstreamattentionwithrotaryembedding_pb_kernel(
 
         def copy_qk(r):
             qk_t[r] = stage.tile([P, 2 * SEQ], BF16, name="qk_t", bufs=3)
-            nc.scalar.copy(out=qk_t[r][:], in_=qk_flipped[r][:])
+            nc.vector.tensor_copy(out=qk_t[r][:], in_=qk_flipped[r][:])
 
-        def softmax_tile(r, j):
-            if j == 0:
-                row_sums[r] = small.tile([P, TILES], F32, name="row_sums")
+        def score_matmul(r, j):
             scores = ps_scores.tile([P, SEQ], F32, name="scores")
             nc.tensor.matmul(
                 out=scores[:],
@@ -156,10 +158,14 @@ def tile_dualstreamattentionwithrotaryembedding_pb_kernel(
                 start=True,
                 stop=True,
             )
+            s_tiles[(r, j)] = scores
+
+        def max_pass(r, j):
+            scores = s_tiles[(r, j)]
+            u = stage.tile([P, SEQ], F32, name="u", bufs=6)
             shift = small.tile([P, 1], F32, name="shift")
-            scaled = stage.tile([P, SEQ], BF16, name="scaled")
             nc.vector.tensor_scalar(
-                out=scaled[:],
+                out=u[:],
                 in0=scores[:],
                 scalar1=-SCALE,
                 scalar2=None,
@@ -167,43 +173,38 @@ def tile_dualstreamattentionwithrotaryembedding_pb_kernel(
                 op1=ALU.min,
                 accum_out=shift[:],
             )
+            u_tiles[(r, j)] = (u, shift)
+
+        def exp_tile(r, j):
+            if j == 0:
+                row_sums[r] = small.tile([P, TILES], F32, name="row_sums")
+            u, shift = u_tiles[(r, j)]
             e = stage.tile([P, SEQ], BF16, name="e", bufs=6)
             nc.scalar.activation(
                 out=e[:],
-                in_=scores[:],
+                in_=u[:],
                 func=ACT.Exp,
                 bias=shift[:],
-                scale=SCALE,
+                scale=-1.0,
                 accum_out=row_sums[r][:, j : j + 1],
             )
             e_tiles[(r, j)] = e
 
-        def regroup(out, in_):
-            nc.gpsimd.tensor_scalar(
-                out=out.rearrange("p (a m t) -> p a m t", m=P, t=PACK),
-                in0=in_.rearrange("p (a t m) -> p a m t", m=P, t=PACK),
-                scalar1=1.0,
-                scalar2=0.0,
-                op0=ALU.mult,
-                op1=ALU.add,
-            )
-
         def transpose_e(r, j):
-            if j % 2 == 0:
-                e_flipped[(r, j // 2)] = ps_et.tile([P, 2, TILES, P], BF16, name="e_flipped")
             e = e_tiles[(r, j)]
+            flipped = ps_et.tile([P, TILES, P], BF16, name="e_flipped")
             for t in range(TILES):
-                nc.tensor.transpose(
-                    e_flipped[(r, j // 2)][:, j % 2, t, :], e[:, t * P : (t + 1) * P], ident_bf[:]
-                )
+                nc.tensor.transpose(flipped[:, t, :], e[:, t * P : (t + 1) * P], ident_bf[:])
+            e_flipped[(r, j)] = flipped
 
-        def copy_e(r, pair):
-            if pair == 0:
+        def copy_e(r, j):
+            if j == 0:
                 e_grouped[r] = stage.tile([P, SEQ * PACK], BF16, name="e_grouped", align_bytes=64, bufs=3)
-            planes = stage.tile([P, 2 * TILES * P], BF16, name="e_planes", bufs=3)
-            nc.scalar.copy(out=planes[:], in_=e_flipped[(r, pair)][:].rearrange("p a t m -> p (a t m)"))
-            span = 2 * P * PACK
-            regroup(e_grouped[r][:, pair * span : (pair + 1) * span], planes[:])
+            span = P * PACK
+            nc.scalar.copy(
+                out=e_grouped[r][:, j * span : (j + 1) * span].rearrange("p (m t) -> p m t", t=PACK),
+                in_=e_flipped[(r, j)][:].rearrange("p t m -> p m t"),
+            )
 
         def quantise_e(r):
             codes = stage.tile([P, SEQ], U32, name="e_codes", align_bytes=64)
@@ -213,13 +214,10 @@ def tile_dualstreamattentionwithrotaryembedding_pb_kernel(
 
         def regroup_weights(i):
             grouped = stage.tile([P, PASSES * HD * PACK], BF16, name="w_grouped", align_bytes=64)
-            if i % 2 == 0:
-                regroup(grouped[:], w_raw[i][:].rearrange("p g t n -> p (g t n)"))
-            else:
-                nc.vector.tensor_copy(
-                    out=grouped[:].rearrange("p (g n t) -> p g n t", g=PASSES, t=PACK),
-                    in_=w_raw[i][:].rearrange("p g t n -> p g n t"),
-                )
+            nc.vector.tensor_copy(
+                out=grouped[:].rearrange("p (g c i t) -> p g c t i", g=PASSES, i=4, t=PACK),
+                in_=w_raw[i][:].rearrange("p g t (c i) -> p g c t i", i=4),
+            )
             w_grouped[i] = grouped
 
         def quantise_weights(i):
@@ -246,7 +244,7 @@ def tile_dualstreamattentionwithrotaryembedding_pb_kernel(
                     )
             v_acc[r] = acc
 
-        def quantise_values(r):
+        def add_bias(r):
             h = r // BATCH
             grouped = stage.tile([P, HD * PACK], BF16, name="v_grouped", align_bytes=64)
             nc.vector.tensor_tensor(
@@ -255,9 +253,12 @@ def tile_dualstreamattentionwithrotaryembedding_pb_kernel(
                 in1=bias[:, :, h * HD : (h + 1) * HD].rearrange("p t n -> p n t"),
                 op=ALU.add,
             )
+            v_grouped[r] = grouped
+
+        def quantise_values(r):
             codes = stage.tile([P, HD], U32, name="v_codes", align_bytes=64)
             scales = stage.tile([P, HD], U8, name="v_scales", align_bytes=64)
-            nc.vector.quantize_mx(out=codes[:].bitcast(FP8X4), scales=scales[:], in_=grouped[:])
+            nc.vector.quantize_mx(out=codes[:].bitcast(FP8X4), scales=scales[:], in_=v_grouped[r][:])
             v_words[r] = (codes, scales)
 
         def attend(r):
@@ -276,10 +277,13 @@ def tile_dualstreamattentionwithrotaryembedding_pb_kernel(
                 )
             y_acc[r] = acc
 
+        def invert_sums(r):
+            inverse[r] = small.tile([P, TILES], F32, name="inverse")
+            nc.vector.reciprocal(out=inverse[r][:], in_=row_sums[r][:])
+
         def store_output(r):
             h, b = divmod(r, BATCH)
-            inv = small.tile([P, TILES], F32, name="inv")
-            nc.vector.reciprocal(out=inv[:], in_=row_sums[r][:])
+            inv = inverse[r]
             y = stage.tile([P, TILES, HD], F32, name="y", bufs=3)
             nc.vector.tensor_tensor(
                 out=y[:], in0=y_acc[r][:], in1=inv[:].unsqueeze(2).to_broadcast([P, TILES, HD]), op=ALU.mult
@@ -294,27 +298,25 @@ def tile_dualstreamattentionwithrotaryembedding_pb_kernel(
             r, rest = divmod(step - offset, TILES)
             return r if rest == 0 and 0 <= r < ROUNDS else None
 
+        def tile_at(step, offset):
+            return divmod(step - offset, TILES) if 0 <= step - offset < TILES * ROUNDS else None
+
+        ctx.enter_context(tc.manual_schedule())
         transpose_qk(0)
         copy_qk(0)
         for step in range(TILES * ROUNDS + 9):
-            if step < TILES * ROUNDS:
-                softmax_tile(step // TILES, step % TILES)
-
+            tile_now = tile_at(step, 0)
+            if tile_now is not None:
+                score_matmul(tile_now[0], tile_now[1])
             r = round_at(step, 8)
             if r is not None:
                 project_values(r)
             r = round_at(step, 11)
             if r is not None:
                 attend(r)
-
-            if 0 <= step - 3 < TILES * ROUNDS:
-                transpose_e((step - 3) // TILES, (step - 3) % TILES)
-            r = round_at(step, 5)
-            if r is not None:
-                copy_e(r, 0)
-            r = round_at(step, 7)
-            if r is not None:
-                copy_e(r, 1)
+            tile_now = tile_at(step, 3)
+            if tile_now is not None:
+                transpose_e(tile_now[0], tile_now[1])
             r = round_at(step, 2 - TILES)
             if r is not None:
                 transpose_qk(r)
@@ -322,24 +324,38 @@ def tile_dualstreamattentionwithrotaryembedding_pb_kernel(
             if r is not None and r < BATCH:
                 transpose_tokens(r)
 
+            tile_now = tile_at(step, 2)
+            if tile_now is not None:
+                exp_tile(tile_now[0], tile_now[1])
+            tile_now = tile_at(step, 4)
+            if tile_now is not None:
+                copy_e(tile_now[0], tile_now[1])
+
+            tile_now = tile_at(step, 1)
+            if tile_now is not None:
+                max_pass(tile_now[0], tile_now[1])
             r = round_at(step, 12)
             if r is not None:
                 store_output(r)
+            r = round_at(step, 8)
+            if r is not None:
+                invert_sums(r)
             r = round_at(step, 9)
             if r is not None:
-                quantise_values(r)
+                add_bias(r)
+                quantise_e(r)
             r = round_at(step, 10)
             if r is not None:
-                quantise_e(r)
-            r = round_at(step, 3 - TILES)
-            if r is not None:
-                copy_qk(r)
+                quantise_values(r)
             r = round_at(step, 2)
             if r is not None:
                 regroup_weights(r)
             r = round_at(step, 3)
             if r is not None:
                 quantise_weights(r)
+            r = round_at(step, 3 - TILES)
+            if r is not None:
+                copy_qk(r)
             r = round_at(step, 4)
             if r is not None and r < BATCH:
                 quantise_tokens(r)

@@ -37,8 +37,8 @@ def tile_dualstreamattentionwithrotaryembedding_pb_kernel(
         keep = ctx.enter_context(tc.tile_pool(name="keep", bufs=1))
         stage = ctx.enter_context(tc.tile_pool(name="stage", bufs=2))
         small = ctx.enter_context(tc.tile_pool(name="small", bufs=8))
-        ps_scores = ctx.enter_context(tc.psum_pool(name="ps_scores", bufs=3))
-        ps_et = ctx.enter_context(tc.psum_pool(name="ps_et", bufs=3))
+        ps_scores = ctx.enter_context(tc.psum_pool(name="ps_scores", bufs=4))
+        ps_et = ctx.enter_context(tc.psum_pool(name="ps_et", bufs=2))
         ps_misc = ctx.enter_context(tc.psum_pool(name="ps_misc", bufs=2))
 
         q_raw = []
@@ -73,14 +73,14 @@ def tile_dualstreamattentionwithrotaryembedding_pb_kernel(
         nc.scalar.dma_start(out=bias_x[:], in_=bv_x.partition_broadcast(P))
         load_qk(0)
         load_qk(1)
-        load_tokens(0)
         load_weights(0)
         load_qk(2)
+        load_tokens(0)
         load_tokens(1)
         for r in range(3, ROUNDS):
+            load_qk(r)
             if r % BATCH == 1:
                 load_weights(r // BATCH)
-            load_qk(r)
 
         ident_bf = const.tile([P, P], BF16)
         make_identity(nc, ident_bf[:])
@@ -147,7 +147,7 @@ def tile_dualstreamattentionwithrotaryembedding_pb_kernel(
 
         def copy_qk(r):
             qk_t[r] = stage.tile([P, 2 * SEQ], BF16, name="qk_t", bufs=3)
-            nc.vector.tensor_copy(out=qk_t[r][:], in_=qk_flipped[r][:])
+            nc.scalar.copy(out=qk_t[r][:], in_=qk_flipped[r][:])
 
         def score_matmul(r, j):
             scores = ps_scores.tile([P, SEQ], F32, name="scores")
@@ -162,7 +162,7 @@ def tile_dualstreamattentionwithrotaryembedding_pb_kernel(
 
         def max_pass(r, j):
             scores = s_tiles[(r, j)]
-            u = stage.tile([P, SEQ], F32, name="u", bufs=6)
+            u = stage.tile([P, SEQ], F32, name="u", bufs=8)
             shift = small.tile([P, 1], F32, name="shift")
             nc.vector.tensor_scalar(
                 out=u[:],
@@ -179,7 +179,7 @@ def tile_dualstreamattentionwithrotaryembedding_pb_kernel(
             if j == 0:
                 row_sums[r] = small.tile([P, TILES], F32, name="row_sums")
             u, shift = u_tiles[(r, j)]
-            e = stage.tile([P, SEQ], BF16, name="e", bufs=6)
+            e = stage.tile([P, SEQ], BF16, name="e", bufs=8)
             nc.scalar.activation(
                 out=e[:],
                 in_=u[:],
@@ -191,19 +191,23 @@ def tile_dualstreamattentionwithrotaryembedding_pb_kernel(
             e_tiles[(r, j)] = e
 
         def transpose_e(r, j):
+            if j % 2 == 0:
+                e_flipped[(r, j // 2)] = ps_et.tile([P, 2, TILES, P], BF16, name="e_flipped")
             e = e_tiles[(r, j)]
-            flipped = ps_et.tile([P, TILES, P], BF16, name="e_flipped")
             for t in range(TILES):
-                nc.tensor.transpose(flipped[:, t, :], e[:, t * P : (t + 1) * P], ident_bf[:])
-            e_flipped[(r, j)] = flipped
+                nc.tensor.transpose(
+                    e_flipped[(r, j // 2)][:, j % 2, t, :], e[:, t * P : (t + 1) * P], ident_bf[:]
+                )
 
-        def copy_e(r, j):
-            if j == 0:
-                e_grouped[r] = stage.tile([P, SEQ * PACK], BF16, name="e_grouped", align_bytes=64, bufs=3)
-            span = P * PACK
+        def copy_e(r, pair):
+            if pair == 0:
+                e_grouped[r] = stage.tile([P, SEQ * PACK], BF16, name="e_grouped", align_bytes=64)
+            span = 2 * P * PACK
             nc.scalar.copy(
-                out=e_grouped[r][:, j * span : (j + 1) * span].rearrange("p (m t) -> p m t", t=PACK),
-                in_=e_flipped[(r, j)][:].rearrange("p t m -> p m t"),
+                out=e_grouped[r][:, pair * span : (pair + 1) * span].rearrange(
+                    "p (a m t) -> p a m t", a=2, t=PACK
+                ),
+                in_=e_flipped[(r, pair)][:].rearrange("p a t m -> p a m t"),
             )
 
         def quantise_e(r):
@@ -294,70 +298,50 @@ def tile_dualstreamattentionwithrotaryembedding_pb_kernel(
                 out=out_0[b].rearrange("(j p) d -> p j d", p=P)[:, :, cols], in_=y[:, 1:TILES, :]
             )
 
-        def round_at(step, offset):
-            r, rest = divmod(step - offset, TILES)
-            return r if rest == 0 and 0 <= r < ROUNDS else None
-
-        def tile_at(step, offset):
-            return divmod(step - offset, TILES) if 0 <= step - offset < TILES * ROUNDS else None
+        def live(r):
+            return 0 <= r < ROUNDS
 
         ctx.enter_context(tc.manual_schedule())
-        transpose_qk(0)
-        copy_qk(0)
-        for step in range(TILES * ROUNDS + 9):
-            tile_now = tile_at(step, 0)
-            if tile_now is not None:
-                score_matmul(tile_now[0], tile_now[1])
-            r = round_at(step, 8)
-            if r is not None:
-                project_values(r)
-            r = round_at(step, 11)
-            if r is not None:
-                attend(r)
-            tile_now = tile_at(step, 3)
-            if tile_now is not None:
-                transpose_e(tile_now[0], tile_now[1])
-            r = round_at(step, 2 - TILES)
-            if r is not None:
-                transpose_qk(r)
-            r = round_at(step, 3)
-            if r is not None and r < BATCH:
-                transpose_tokens(r)
-
-            tile_now = tile_at(step, 2)
-            if tile_now is not None:
-                exp_tile(tile_now[0], tile_now[1])
-            tile_now = tile_at(step, 4)
-            if tile_now is not None:
-                copy_e(tile_now[0], tile_now[1])
-
-            tile_now = tile_at(step, 1)
-            if tile_now is not None:
-                max_pass(tile_now[0], tile_now[1])
-            r = round_at(step, 12)
-            if r is not None:
-                store_output(r)
-            r = round_at(step, 8)
-            if r is not None:
-                invert_sums(r)
-            r = round_at(step, 9)
-            if r is not None:
-                add_bias(r)
-                quantise_e(r)
-            r = round_at(step, 10)
-            if r is not None:
-                quantise_values(r)
-            r = round_at(step, 2)
-            if r is not None:
-                regroup_weights(r)
-            r = round_at(step, 3)
-            if r is not None:
-                quantise_weights(r)
-            r = round_at(step, 3 - TILES)
-            if r is not None:
-                copy_qk(r)
-            r = round_at(step, 4)
-            if r is not None and r < BATCH:
-                quantise_tokens(r)
-            if step == 5:
+        for k in range(-2, ROUNDS + 4):
+            if live(k + 1):
+                copy_qk(k + 1)
+            if live(k - 2):
+                project_values(k - 2)
+            if live(k - 3):
+                attend(k - 3)
+            if live(k):
+                for j in range(TILES):
+                    max_pass(k, j)
+            if live(k + 1):
+                for j in range(TILES):
+                    score_matmul(k + 1, j)
+            if live(k - 2):
+                copy_e(k - 2, 0)
+                copy_e(k - 2, 1)
+            if live(k - 1):
+                for j in range(TILES):
+                    transpose_e(k - 1, j)
+            if live(k):
+                regroup_weights(k)
+            if live(k - 2):
+                add_bias(k - 2)
+            if live(k):
+                for j in range(TILES):
+                    exp_tile(k, j)
+            if 0 <= k < BATCH:
+                transpose_tokens(k)
+            if live(k + 2):
+                transpose_qk(k + 2)
+            if live(k - 3):
+                store_output(k - 3)
+            if live(k - 2):
+                quantise_e(k - 2)
+                quantise_values(k - 2)
+            if live(k):
+                quantise_weights(k)
+            if live(k - 1):
+                invert_sums(k - 1)
+            if 0 <= k - 1 < BATCH:
+                quantise_tokens(k - 1)
+            if k == 1:
                 spread_bias()

@@ -87,6 +87,10 @@ def tile_dualstreamattentionwithrotaryembedding_pb_kernel(
         ident_f32 = const.tile([P, P], F32)
         make_identity(nc, ident_f32[:])
 
+        warm = const.tile([P, 1], F32)
+        nc.vector.memset(warm[:], 0.0)
+        nc.scalar.activation(out=warm[:], in_=warm[:], func=ACT.Exp)
+
         tok_codes = [keep.tile([P, TILES * PASSES * P], U32, name="tok_codes%d" % b, align_bytes=64) for b in range(BATCH)]
         tok_scales = [keep.tile([P, TILES * PASSES * P], U8, name="tok_scales%d" % b, align_bytes=64) for b in range(BATCH)]
         w_codes = [keep.tile([P, PASSES * HD], U32, name="w_codes%d" % i, align_bytes=64) for i in range(2 * HEADS)]
@@ -302,9 +306,7 @@ def tile_dualstreamattentionwithrotaryembedding_pb_kernel(
             return 0 <= r < ROUNDS
 
         ctx.enter_context(tc.manual_schedule())
-        for k in range(-2, ROUNDS + 4):
-            if live(k + 1):
-                copy_qk(k + 1)
+        for k in range(-3, ROUNDS + 4):
             if live(k - 2):
                 project_values(k - 2)
             if live(k - 3):
@@ -321,24 +323,25 @@ def tile_dualstreamattentionwithrotaryembedding_pb_kernel(
             if live(k - 1):
                 for j in range(TILES):
                     transpose_e(k - 1, j)
-            if live(k):
-                regroup_weights(k)
+            if live(k + 1):
+                regroup_weights(k + 1)
             if live(k - 2):
                 add_bias(k - 2)
             if live(k):
                 for j in range(TILES):
                     exp_tile(k, j)
-            if 0 <= k < BATCH:
-                transpose_tokens(k)
             if live(k + 2):
                 transpose_qk(k + 2)
+                copy_qk(k + 2)
+            if 0 <= k < BATCH:
+                transpose_tokens(k)
             if live(k - 3):
                 store_output(k - 3)
             if live(k - 2):
                 quantise_e(k - 2)
                 quantise_values(k - 2)
-            if live(k):
-                quantise_weights(k)
+            if live(k + 1):
+                quantise_weights(k + 1)
             if live(k - 1):
                 invert_sums(k - 1)
             if 0 <= k - 1 < BATCH:

@@ -169,8 +169,8 @@ def tile_dualstreamattentionwithrotaryembedding_pb_kernel(
             u = stage.tile([P, SEQ], F32, name="u", bufs=8)
             shift = small.tile([P, 1], F32, name="shift")
             nc.vector.tensor_scalar(
-                out=u[:],
-                in0=scores[:],
+                out=u[:].rearrange("p (v m w) -> p v m w", v=2, w=2),
+                in0=scores[:].rearrange("p (v w m) -> p v m w", v=2, w=2),
                 scalar1=-SCALE,
                 scalar2=None,
                 op0=ALU.mult,
@@ -196,11 +196,11 @@ def tile_dualstreamattentionwithrotaryembedding_pb_kernel(
 
         def transpose_e(r, j):
             if j % 2 == 0:
-                e_flipped[(r, j // 2)] = ps_et.tile([P, 2, TILES, P], BF16, name="e_flipped")
-            e = e_tiles[(r, j)]
-            for t in range(TILES):
+                e_flipped[(r, j // 2)] = ps_et.tile([P, 2, TILES // 2, P], F32, name="e_flipped")
+            words = e_tiles[(r, j)][:].bitcast(F32)
+            for v in range(TILES // 2):
                 nc.tensor.transpose(
-                    e_flipped[(r, j // 2)][:, j % 2, t, :], e[:, t * P : (t + 1) * P], ident_bf[:]
+                    e_flipped[(r, j // 2)][:, j % 2, v, :], words[:, v * P : (v + 1) * P], ident_f32[:]
                 )
 
         def copy_e(r, pair):
@@ -208,10 +208,10 @@ def tile_dualstreamattentionwithrotaryembedding_pb_kernel(
                 e_grouped[r] = stage.tile([P, SEQ * PACK], BF16, name="e_grouped", align_bytes=64)
             span = 2 * P * PACK
             nc.scalar.copy(
-                out=e_grouped[r][:, pair * span : (pair + 1) * span].rearrange(
-                    "p (a m t) -> p a m t", a=2, t=PACK
-                ),
-                in_=e_flipped[(r, pair)][:].rearrange("p a t m -> p a m t"),
+                out=e_grouped[r][:, pair * span : (pair + 1) * span]
+                .bitcast(F32)
+                .rearrange("p (a m v) -> p a m v", a=2, v=TILES // 2),
+                in_=e_flipped[(r, pair)][:].rearrange("p a v m -> p a m v"),
             )
 
         def quantise_e(r):

@@ -293,9 +293,10 @@ def tile_dualstreamattentionwithrotaryembedding_pb_kernel(
             h, b = divmod(r, BATCH)
             inv = inverse[r]
             y = stage.tile([P, TILES, HD], F32, name="y", bufs=3)
-            nc.vector.tensor_tensor(
-                out=y[:], in0=y_acc[r][:], in1=inv[:].unsqueeze(2).to_broadcast([P, TILES, HD]), op=ALU.mult
-            )
+            for j in range(TILES):
+                nc.scalar.activation(
+                    out=y[:, j, :], in_=y_acc[r][:, j, :], func=ACT.Copy, scale=inv[:, j : j + 1]
+                )
             cols = slice(h * HD, (h + 1) * HD)
             nc.sync.dma_start(out=out_1[b, :, cols], in_=y[:, 0, :])
             nc.sync.dma_start(
@@ -327,16 +328,16 @@ def tile_dualstreamattentionwithrotaryembedding_pb_kernel(
                 regroup_weights(k + 1)
             if live(k - 2):
                 add_bias(k - 2)
-            if live(k):
-                for j in range(TILES):
+            for j in range(TILES):
+                if live(k):
                     exp_tile(k, j)
+                if j == 1 and live(k - 3):
+                    store_output(k - 3)
             if live(k + 2):
                 transpose_qk(k + 2)
                 copy_qk(k + 2)
             if 0 <= k < BATCH:
                 transpose_tokens(k)
-            if live(k - 3):
-                store_output(k - 3)
             if live(k - 2):
                 quantise_e(k - 2)
                 quantise_values(k - 2)

@@ -23,6 +23,7 @@ TILES = SEQ // P
 PASSES = D // (P * PACK)
 ROUNDS = BATCH * HEADS
 SCALE = 1.0 / math.sqrt(HD)
+Y_ON_VECTOR = 2
 
 FLOPS = 2 * BATCH * SEQ * D * D + 2 * 2 * ROUNDS * SEQ * SEQ * HD
 
@@ -222,9 +223,13 @@ def tile_dualstreamattentionwithrotaryembedding_pb_kernel(
 
         def regroup_weights(i):
             grouped = stage.tile([P, PASSES * HD * PACK], BF16, name="w_grouped", align_bytes=64)
-            nc.vector.tensor_copy(
-                out=grouped[:].rearrange("p (g c i t) -> p g c t i", g=PASSES, i=4, t=PACK),
-                in_=w_raw[i][:].rearrange("p g t (c i) -> p g c t i", i=4),
+            nc.gpsimd.tensor_scalar(
+                out=grouped[:].rearrange("p (g n t) -> p g n t", g=PASSES, t=PACK),
+                in0=w_raw[i][:].rearrange("p g t n -> p g n t"),
+                scalar1=1.0,
+                scalar2=0.0,
+                op0=ALU.mult,
+                op1=ALU.add,
             )
             w_grouped[i] = grouped
 
@@ -293,7 +298,13 @@ def tile_dualstreamattentionwithrotaryembedding_pb_kernel(
             h, b = divmod(r, BATCH)
             inv = inverse[r]
             y = stage.tile([P, TILES, HD], F32, name="y", bufs=3)
-            for j in range(TILES):
+            nc.vector.tensor_tensor(
+                out=y[:, :Y_ON_VECTOR, :],
+                in0=y_acc[r][:, :Y_ON_VECTOR, :],
+                in1=inv[:, :Y_ON_VECTOR].unsqueeze(2).to_broadcast([P, Y_ON_VECTOR, HD]),
+                op=ALU.mult,
+            )
+            for j in range(Y_ON_VECTOR, TILES):
                 nc.scalar.activation(
                     out=y[:, j, :], in_=y_acc[r][:, j, :], func=ACT.Copy, scale=inv[:, j : j + 1]
                 )

@@ -24,6 +24,7 @@ PASSES = D // (P * PACK)
 ROUNDS = BATCH * HEADS
 SCALE = 1.0 / math.sqrt(HD)
 Y_ON_VECTOR = 2
+SCORE_BANKS = 4
 
 FLOPS = 2 * BATCH * SEQ * D * D + 2 * 2 * ROUNDS * SEQ * SEQ * HD
 
@@ -38,7 +39,7 @@ def tile_dualstreamattentionwithrotaryembedding_pb_kernel(
         keep = ctx.enter_context(tc.tile_pool(name="keep", bufs=1))
         stage = ctx.enter_context(tc.tile_pool(name="stage", bufs=2))
         small = ctx.enter_context(tc.tile_pool(name="small", bufs=8))
-        ps_scores = ctx.enter_context(tc.psum_pool(name="ps_scores", bufs=4))
+        ps_scores = ctx.enter_context(tc.psum_pool(name="ps_scores", bufs=SCORE_BANKS))
         ps_et = ctx.enter_context(tc.psum_pool(name="ps_et", bufs=2))
         ps_misc = ctx.enter_context(tc.psum_pool(name="ps_misc", bufs=2))
 
@@ -48,7 +49,7 @@ def tile_dualstreamattentionwithrotaryembedding_pb_kernel(
             q_raw.append(raw.tile([P, TILES, HD], BF16, name="q_raw%d" % r))
             k_raw.append(raw.tile([P, TILES, HD], BF16, name="k_raw%d" % r))
         tok_raw = [raw.tile([P, TILES, D], BF16, name="tok_raw%d" % b) for b in range(BATCH)]
-        w_raw = [raw.tile([P, PASSES, PACK, HD], BF16, name="w_raw%d" % i) for i in range(2 * HEADS)]
+        w_raw = [raw.tile([P, PASSES, PACK, 2 * HD], BF16, name="w_raw%d" % i) for i in range(HEADS)]
         bias_x = const.tile([P, D], BF16)
         bias = const.tile([P, TILES, D], BF16)
 
@@ -63,25 +64,27 @@ def tile_dualstreamattentionwithrotaryembedding_pb_kernel(
                 out=tok_raw[b][:, 1:TILES, :], in_=x[b].rearrange("(j p) k -> p j k", p=P)
             )
 
-        def load_weights(h):
+        def load_weights(pair):
             for w, weights in enumerate((Wv_c, Wv_x)):
                 rows = weights.rearrange("(a p e) n -> p a e n", p=P, e=2)
-                slots = w_raw[2 * h + w][:].rearrange("p g (u e) n -> p (g u) e n", e=2)
+                slots = w_raw[2 * pair + w][:].rearrange("p g (u e) n -> p (g u) e n", e=2)
+                cols = slice(2 * pair * HD, 2 * (pair + 1) * HD)
                 for e in range(2):
-                    nc.sync.dma_start(out=slots[:, :, e, :], in_=rows[:, :, e, h * HD : (h + 1) * HD])
+                    nc.sync.dma_start(out=slots[:, :, e, :], in_=rows[:, :, e, cols])
 
-        nc.scalar.dma_start(out=bias[:, 0, :], in_=bv_c.partition_broadcast(P))
-        nc.scalar.dma_start(out=bias_x[:], in_=bv_x.partition_broadcast(P))
         load_qk(0)
         load_qk(1)
-        load_weights(0)
-        load_qk(2)
         load_tokens(0)
+        load_qk(2)
+        load_weights(0)
+        load_qk(3)
         load_tokens(1)
-        for r in range(3, ROUNDS):
+        nc.sync.dma_start(out=bias[:, 0, :], in_=bv_c.partition_broadcast(P))
+        nc.sync.dma_start(out=bias_x[:], in_=bv_x.partition_broadcast(P))
+        for r in range(4, ROUNDS):
             load_qk(r)
-            if r % BATCH == 1:
-                load_weights(r // BATCH)
+            if r % 4 == 0:
+                load_weights(r // 4)
 
         ident_bf = const.tile([P, P], BF16)
         make_identity(nc, ident_bf[:])
@@ -111,17 +114,20 @@ def tile_dualstreamattentionwithrotaryembedding_pb_kernel(
         v_words = {}
         v_acc = {}
         y_acc = {}
+        y_tiles = {}
         row_sums = {}
 
-        def transpose_tokens(b):
-            tok_grouped[b] = stage.tile([P, TILES * PASSES * P * PACK], BF16, name="tok_grouped", align_bytes=64)
-            for t in range(TILES):
+        def transpose_tokens(b, tiles):
+            if b not in tok_grouped:
+                tok_grouped[b] = stage.tile([P, TILES * PASSES * P * PACK], BF16, name="tok_grouped", align_bytes=64)
+            for t in tiles:
                 words = tok_raw[b][:, t, :].bitcast(F32)
-                flipped = ps_misc.tile([P, PASSES * 2, P], F32, name="tok_flipped", tag="misc")
+                flipped = ps_et.tile([P, PASSES * 2, P], F32, name="tok_flipped", tag="e_flipped")
                 for a in range(PASSES * 2):
                     nc.tensor.transpose(flipped[:, a, :], words[:, a * P : (a + 1) * P], ident_f32[:])
                 span = PASSES * P * PACK
-                nc.scalar.copy(
+                copy = nc.scalar.copy if t % 2 == 0 else nc.vector.tensor_copy
+                copy(
                     out=tok_grouped[b][:, t * span : (t + 1) * span]
                     .bitcast(F32)
                     .rearrange("p (g m u) -> p g m u", g=PASSES, u=2),
@@ -133,9 +139,15 @@ def tile_dualstreamattentionwithrotaryembedding_pb_kernel(
                 out=tok_codes[b][:].bitcast(FP8X4), scales=tok_scales[b][:], in_=tok_grouped[b][:]
             )
 
-        def spread_bias():
-            nc.vector.tensor_copy(
-                out=bias[:, 1:TILES, :], in_=bias_x[:].unsqueeze(1).to_broadcast([P, TILES - 1, D])
+        def spread_bias(h):
+            cols = slice(h * HD, (h + 1) * HD)
+            nc.gpsimd.tensor_scalar(
+                out=bias[:, 1:TILES, cols],
+                in0=bias_x[:, cols].unsqueeze(1).to_broadcast([P, TILES - 1, HD]),
+                scalar1=1.0,
+                scalar2=0.0,
+                op0=ALU.mult,
+                op1=ALU.add,
             )
 
         qk_flipped = {}
@@ -152,7 +164,11 @@ def tile_dualstreamattentionwithrotaryembedding_pb_kernel(
 
         def copy_qk(r):
             qk_t[r] = stage.tile([P, 2 * SEQ], BF16, name="qk_t", bufs=3)
-            nc.scalar.copy(out=qk_t[r][:], in_=qk_flipped[r][:])
+            if r == 0:
+                nc.vector.tensor_copy(out=qk_t[r][:, :SEQ], in_=qk_flipped[r][:, :SEQ])
+                nc.scalar.copy(out=qk_t[r][:, SEQ:], in_=qk_flipped[r][:, SEQ:])
+            else:
+                nc.scalar.copy(out=qk_t[r][:], in_=qk_flipped[r][:])
 
         def score_matmul(r, j):
             scores = ps_scores.tile([P, SEQ], F32, name="scores")
@@ -167,7 +183,7 @@ def tile_dualstreamattentionwithrotaryembedding_pb_kernel(
 
         def max_pass(r, j):
             scores = s_tiles[(r, j)]
-            u = stage.tile([P, SEQ], F32, name="u", bufs=8)
+            u = stage.tile([P, SEQ], F32, name="u", bufs=12)
             shift = small.tile([P, 1], F32, name="shift")
             nc.vector.tensor_scalar(
                 out=u[:].rearrange("p (v m w) -> p v m w", v=2, w=2),
@@ -181,7 +197,7 @@ def tile_dualstreamattentionwithrotaryembedding_pb_kernel(
             u_tiles[(r, j)] = (u, shift)
 
         def exp_tile(r, j):
-            if j == 0:
+            if r not in row_sums:
                 row_sums[r] = small.tile([P, TILES], F32, name="row_sums")
             u, shift = u_tiles[(r, j)]
             e = stage.tile([P, SEQ], BF16, name="e", bufs=8)
@@ -196,7 +212,7 @@ def tile_dualstreamattentionwithrotaryembedding_pb_kernel(
             e_tiles[(r, j)] = e
 
         def transpose_e(r, j):
-            if j % 2 == 0:
+            if (r, j // 2) not in e_flipped:
                 e_flipped[(r, j // 2)] = ps_et.tile([P, 2, TILES // 2, P], F32, name="e_flipped")
             words = e_tiles[(r, j)][:].bitcast(F32)
             for v in range(TILES // 2):
@@ -204,11 +220,11 @@ def tile_dualstreamattentionwithrotaryembedding_pb_kernel(
                     e_flipped[(r, j // 2)][:, j % 2, v, :], words[:, v * P : (v + 1) * P], ident_f32[:]
                 )
 
-        def copy_e(r, pair):
-            if pair == 0:
+        def copy_e(r, pair, copy=nc.scalar.copy):
+            if r not in e_grouped:
                 e_grouped[r] = stage.tile([P, SEQ * PACK], BF16, name="e_grouped", align_bytes=64)
             span = 2 * P * PACK
-            nc.scalar.copy(
+            copy(
                 out=e_grouped[r][:, pair * span : (pair + 1) * span]
                 .bitcast(F32)
                 .rearrange("p (a m v) -> p a m v", a=2, v=TILES // 2),
@@ -216,8 +232,8 @@ def tile_dualstreamattentionwithrotaryembedding_pb_kernel(
             )
 
         def quantise_e(r):
-            codes = stage.tile([P, SEQ], U32, name="e_codes", align_bytes=64)
-            scales = stage.tile([P, SEQ], U8, name="e_scales", align_bytes=64)
+            codes = stage.tile([P, SEQ], U32, name="e_codes", align_bytes=64, bufs=4)
+            scales = stage.tile([P, SEQ], U8, name="e_scales", align_bytes=64, bufs=4)
             nc.vector.quantize_mx(out=codes[:].bitcast(FP8X4), scales=scales[:], in_=e_grouped[r][:])
             e_words[r] = (codes, scales)
 
@@ -225,7 +241,9 @@ def tile_dualstreamattentionwithrotaryembedding_pb_kernel(
             grouped = stage.tile([P, PASSES * HD * PACK], BF16, name="w_grouped", align_bytes=64)
             nc.gpsimd.tensor_scalar(
                 out=grouped[:].rearrange("p (g n t) -> p g n t", g=PASSES, t=PACK),
-                in0=w_raw[i][:].rearrange("p g t n -> p g n t"),
+                in0=w_raw[2 * (i // 4) + i % 2][:, :, :, (i // 2 % 2) * HD : (i // 2 % 2 + 1) * HD].rearrange(
+                    "p g t n -> p g n t"
+                ),
                 scalar1=1.0,
                 scalar2=0.0,
                 op0=ALU.mult,
@@ -259,7 +277,7 @@ def tile_dualstreamattentionwithrotaryembedding_pb_kernel(
 
         def add_bias(r):
             h = r // BATCH
-            grouped = stage.tile([P, HD * PACK], BF16, name="v_grouped", align_bytes=64)
+            grouped = stage.tile([P, HD * PACK], BF16, name="v_grouped", align_bytes=64, bufs=3)
             nc.vector.tensor_tensor(
                 out=grouped[:].rearrange("p (n t) -> p n t", t=PACK),
                 in0=v_acc[r][:].rearrange("p t n -> p n t"),
@@ -269,8 +287,8 @@ def tile_dualstreamattentionwithrotaryembedding_pb_kernel(
             v_grouped[r] = grouped
 
         def quantise_values(r):
-            codes = stage.tile([P, HD], U32, name="v_codes", align_bytes=64)
-            scales = stage.tile([P, HD], U8, name="v_scales", align_bytes=64)
+            codes = stage.tile([P, HD], U32, name="v_codes", align_bytes=64, bufs=3)
+            scales = stage.tile([P, HD], U8, name="v_scales", align_bytes=64, bufs=3)
             nc.vector.quantize_mx(out=codes[:].bitcast(FP8X4), scales=scales[:], in_=v_grouped[r][:])
             v_words[r] = (codes, scales)
 
@@ -294,20 +312,27 @@ def tile_dualstreamattentionwithrotaryembedding_pb_kernel(
             inverse[r] = small.tile([P, TILES], F32, name="inverse")
             nc.vector.reciprocal(out=inverse[r][:], in_=row_sums[r][:])
 
+        def scale_output(r, tiles, on_vector):
+            if r not in y_tiles:
+                y_tiles[r] = stage.tile([P, TILES, HD], F32, name="y", bufs=3)
+            y = y_tiles[r]
+            inv = inverse[r]
+            if on_vector:
+                nc.vector.tensor_tensor(
+                    out=y[:, tiles, :],
+                    in0=y_acc[r][:, tiles, :],
+                    in1=inv[:, tiles].unsqueeze(2).to_broadcast([P, tiles.stop - tiles.start, HD]),
+                    op=ALU.mult,
+                )
+            else:
+                for j in range(tiles.start, tiles.stop):
+                    nc.scalar.activation(
+                        out=y[:, j, :], in_=y_acc[r][:, j, :], func=ACT.Copy, scale=inv[:, j : j + 1]
+                    )
+
         def store_output(r):
             h, b = divmod(r, BATCH)
-            inv = inverse[r]
-            y = stage.tile([P, TILES, HD], F32, name="y", bufs=3)
-            nc.vector.tensor_tensor(
-                out=y[:, :Y_ON_VECTOR, :],
-                in0=y_acc[r][:, :Y_ON_VECTOR, :],
-                in1=inv[:, :Y_ON_VECTOR].unsqueeze(2).to_broadcast([P, Y_ON_VECTOR, HD]),
-                op=ALU.mult,
-            )
-            for j in range(Y_ON_VECTOR, TILES):
-                nc.scalar.activation(
-                    out=y[:, j, :], in_=y_acc[r][:, j, :], func=ACT.Copy, scale=inv[:, j : j + 1]
-                )
+            y = y_tiles[r]
             cols = slice(h * HD, (h + 1) * HD)
             nc.sync.dma_start(out=out_1[b, :, cols], in_=y[:, 0, :])
             nc.sync.dma_start(
@@ -318,45 +343,100 @@ def tile_dualstreamattentionwithrotaryembedding_pb_kernel(
             return 0 <= r < ROUNDS
 
         ctx.enter_context(tc.manual_schedule())
-        for k in range(-3, ROUNDS + 4):
+
+        transpose_qk(0)
+        copy_qk(0)
+        score_matmul(0, 0)
+        score_matmul(0, 1)
+        transpose_qk(1)
+        score_matmul(0, 2)
+        score_matmul(0, 3)
+        for j in (0, 1):
+            max_pass(0, j)
+            exp_tile(0, j)
+        copy_qk(1)
+        for j in (2, 3):
+            max_pass(0, j)
+            exp_tile(0, j)
+        transpose_tokens(0, (0, 1))
+        for j in range(TILES):
+            score_matmul(1, j)
+            max_pass(1, j)
+        exp_tile(1, 0)
+        exp_tile(1, 1)
+        transpose_tokens(0, (2, 3))
+        transpose_qk(2)
+        copy_qk(2)
+        exp_tile(1, 2)
+        exp_tile(1, 3)
+        for j in range(TILES):
+            transpose_e(0, j)
+        copy_e(0, 0)
+        copy_e(0, 1)
+        for j in range(TILES):
+            score_matmul(2, j)
+        regroup_weights(0)
+        regroup_weights(1)
+        spread_bias(0)
+        spread_bias(1)
+        quantise_tokens(0)
+        quantise_weights(0)
+        quantise_weights(1)
+        regroup_weights(2)
+        regroup_weights(3)
+        transpose_tokens(1, (0, 1))
+        transpose_qk(3)
+        copy_qk(3)
+
+        for k in range(2, ROUNDS + 4):
             if live(k - 2):
                 project_values(k - 2)
+                if k > 2:
+                    copy_e(k - 2, 0)
+                    copy_e(k - 2, 1)
+            if live(k):
+                max_pass(k, 3)
+            for j in (0, 1, 2):
+                if live(k):
+                    max_pass(k, j)
+                if live(k + 1):
+                    score_matmul(k + 1, j)
+            if live(k + 1):
+                score_matmul(k + 1, 3)
             if live(k - 3):
                 attend(k - 3)
+            if k == 2:
+                transpose_tokens(1, (2, 3))
             if live(k):
-                for j in range(TILES):
-                    max_pass(k, j)
-            if live(k + 1):
-                for j in range(TILES):
-                    score_matmul(k + 1, j)
-            if live(k - 2):
-                copy_e(k - 2, 0)
-                copy_e(k - 2, 1)
-            if live(k - 1):
-                for j in range(TILES):
-                    transpose_e(k - 1, j)
-            if live(k + 1):
-                regroup_weights(k + 1)
+                exp_tile(k, 0)
+                exp_tile(k, 3)
             if live(k - 2):
                 add_bias(k - 2)
-            for j in range(TILES):
-                if live(k):
-                    exp_tile(k, j)
-                if j == 1 and live(k - 3):
-                    store_output(k - 3)
+                quantise_e(k - 2)
+            if live(k - 3):
+                scale_output(k - 3, slice(Y_ON_VECTOR, TILES), False)
+            if live(k):
+                exp_tile(k, 2)
+                exp_tile(k, 1)
+            if k == 2:
+                quantise_tokens(1)
+            if live(k - 2):
+                quantise_values(k - 2)
+            if live(k - 3):
+                scale_output(k - 3, slice(0, Y_ON_VECTOR), True)
+                store_output(k - 3)
+            if live(k):
+                quantise_weights(k)
+            if live(k + 2):
+                regroup_weights(k + 2)
+                if k % 2 == 0:
+                    spread_bias(k // 2 + 1)
+            if k == 2:
+                invert_sums(0)
+            if live(k - 1):
+                invert_sums(k - 1)
+                for j in (0, 1, 2, 3):
+                    transpose_e(k - 1, j)
             if live(k + 2):
                 transpose_qk(k + 2)
                 copy_qk(k + 2)
-            if 0 <= k < BATCH:
-                transpose_tokens(k)
-            if live(k - 2):
-                quantise_e(k - 2)
-                quantise_values(k - 2)
-            if live(k + 1):
-                quantise_weights(k + 1)
-            if live(k - 1):
-                invert_sums(k - 1)
-            if 0 <= k - 1 < BATCH:
-                quantise_tokens(k - 1)
-            if k == 1:
-                spread_bias()

@@ -100,6 +100,7 @@ def tile_dualstreamattentionwithrotaryembedding_pb_kernel(
         w_codes = [keep.tile([P, PASSES * HD], U32, name="w_codes%d" % i, align_bytes=64) for i in range(2 * HEADS)]
         w_scales = [keep.tile([P, PASSES * HD], U8, name="w_scales%d" % i, align_bytes=64) for i in range(2 * HEADS)]
 
+        tok_flipped = {}
         tok_grouped = {}
         qk_t = {}
         s_tiles = {}
@@ -117,22 +118,23 @@ def tile_dualstreamattentionwithrotaryembedding_pb_kernel(
         y_tiles = {}
         row_sums = {}
 
-        def transpose_tokens(b, tiles):
+        def transpose_tokens(b, t, pool, tag):
+            words = tok_raw[b][:, t, :].bitcast(F32)
+            flipped = pool.tile([P, PASSES * 2, P], F32, name="tok_flipped", tag=tag)
+            for a in range(PASSES * 2):
+                nc.tensor.transpose(flipped[:, a, :], words[:, a * P : (a + 1) * P], ident_f32[:])
+            tok_flipped[(b, t)] = flipped
+
+        def copy_tokens(b, t, copy):
             if b not in tok_grouped:
                 tok_grouped[b] = stage.tile([P, TILES * PASSES * P * PACK], BF16, name="tok_grouped", align_bytes=64)
-            for t in tiles:
-                words = tok_raw[b][:, t, :].bitcast(F32)
-                flipped = ps_et.tile([P, PASSES * 2, P], F32, name="tok_flipped", tag="e_flipped")
-                for a in range(PASSES * 2):
-                    nc.tensor.transpose(flipped[:, a, :], words[:, a * P : (a + 1) * P], ident_f32[:])
-                span = PASSES * P * PACK
-                copy = nc.scalar.copy if t % 2 == 0 else nc.vector.tensor_copy
-                copy(
-                    out=tok_grouped[b][:, t * span : (t + 1) * span]
-                    .bitcast(F32)
-                    .rearrange("p (g m u) -> p g m u", g=PASSES, u=2),
-                    in_=flipped[:].rearrange("p (g u) m -> p g m u", u=2),
-                )
+            span = PASSES * P * PACK
+            copy(
+                out=tok_grouped[b][:, t * span : (t + 1) * span]
+                .bitcast(F32)
+                .rearrange("p (g m u) -> p g m u", g=PASSES, u=2),
+                in_=tok_flipped[(b, t)][:].rearrange("p (g u) m -> p g m u", u=2),
+            )
 
         def quantise_tokens(b):
             nc.vector.quantize_mx(
@@ -317,7 +319,9 @@ def tile_dualstreamattentionwithrotaryembedding_pb_kernel(
                 y_tiles[r] = stage.tile([P, TILES, HD], F32, name="y", bufs=3)
             y = y_tiles[r]
             inv = inverse[r]
-            if on_vector:
+            if tiles.stop == tiles.start:
+                pass
+            elif on_vector:
                 nc.vector.tensor_tensor(
                     out=y[:, tiles, :],
                     in0=y_acc[r][:, tiles, :],
@@ -325,7 +329,7 @@ def tile_dualstreamattentionwithrotaryembedding_pb_kernel(
                     op=ALU.mult,
                 )
             else:
-                for j in range(tiles.start, tiles.stop):
+                for j in reversed(range(tiles.start, tiles.stop)):
                     nc.scalar.activation(
                         out=y[:, j, :], in_=y_acc[r][:, j, :], func=ACT.Copy, scale=inv[:, j : j + 1]
                     )
@@ -343,6 +347,7 @@ def tile_dualstreamattentionwithrotaryembedding_pb_kernel(
             return 0 <= r < ROUNDS
 
         ctx.enter_context(tc.manual_schedule())
+        on_scalar, on_vector = nc.scalar.copy, nc.vector.tensor_copy
 
         transpose_qk(0)
         copy_qk(0)
@@ -358,23 +363,29 @@ def tile_dualstreamattentionwithrotaryembedding_pb_kernel(
         for j in (2, 3):
             max_pass(0, j)
             exp_tile(0, j)
-        transpose_tokens(0, (0, 1))
+        transpose_tokens(0, 0, ps_et, "e_flipped")
+        copy_tokens(0, 0, on_scalar)
+        transpose_tokens(0, 1, ps_et, "e_flipped")
+        copy_tokens(0, 1, on_vector)
         for j in range(TILES):
             score_matmul(1, j)
             max_pass(1, j)
         exp_tile(1, 0)
         exp_tile(1, 1)
-        transpose_tokens(0, (2, 3))
+        transpose_tokens(0, 2, ps_et, "e_flipped")
+        copy_tokens(0, 2, on_scalar)
+        transpose_tokens(0, 3, ps_et, "e_flipped")
+        copy_tokens(0, 3, on_vector)
         transpose_qk(2)
         copy_qk(2)
         exp_tile(1, 2)
         exp_tile(1, 3)
         for j in range(TILES):
             transpose_e(0, j)
-        copy_e(0, 0)
         copy_e(0, 1)
-        for j in range(TILES):
-            score_matmul(2, j)
+        copy_e(0, 0)
+        transpose_tokens(1, 0, ps_misc, "misc")
+        copy_tokens(1, 0, on_scalar)
         regroup_weights(0)
         regroup_weights(1)
         spread_bias(0)
@@ -384,44 +395,54 @@ def tile_dualstreamattentionwithrotaryembedding_pb_kernel(
         quantise_weights(1)
         regroup_weights(2)
         regroup_weights(3)
-        transpose_tokens(1, (0, 1))
+        transpose_tokens(1, 1, ps_misc, "misc")
+        copy_tokens(1, 1, on_vector)
+        for j in range(TILES):
+            score_matmul(2, j)
+            max_pass(2, j)
         transpose_qk(3)
         copy_qk(3)
+        transpose_tokens(1, 2, ps_et, "e_flipped")
+        copy_tokens(1, 2, on_scalar)
+        transpose_tokens(1, 3, ps_et, "e_flipped")
+        copy_tokens(1, 3, on_vector)
 
-        for k in range(2, ROUNDS + 4):
+        for k in range(2, ROUNDS):
             if live(k - 2):
                 project_values(k - 2)
                 if k > 2:
-                    copy_e(k - 2, 0)
                     copy_e(k - 2, 1)
-            if live(k):
+                    copy_e(k - 2, 0)
+            if k > 2:
                 max_pass(k, 3)
             for j in (0, 1, 2):
-                if live(k):
+                if k > 2:
                     max_pass(k, j)
                 if live(k + 1):
                     score_matmul(k + 1, j)
             if live(k + 1):
                 score_matmul(k + 1, 3)
-            if live(k - 3):
-                attend(k - 3)
-            if k == 2:
-                transpose_tokens(1, (2, 3))
-            if live(k):
-                exp_tile(k, 0)
-                exp_tile(k, 3)
+            exp_tile(k, 0)
+            exp_tile(k, 3)
+            if k == ROUNDS - 1:
+                exp_tile(k, 2)
+                exp_tile(k, 1)
+                for j in range(TILES):
+                    transpose_e(k - 1, j)
             if live(k - 2):
                 add_bias(k - 2)
+            if live(k - 3):
+                quantise_values(k - 3)
+                attend(k - 3)
+            if live(k - 2):
                 quantise_e(k - 2)
             if live(k - 3):
                 scale_output(k - 3, slice(Y_ON_VECTOR, TILES), False)
-            if live(k):
+            if k < ROUNDS - 1:
                 exp_tile(k, 2)
                 exp_tile(k, 1)
             if k == 2:
                 quantise_tokens(1)
-            if live(k - 2):
-                quantise_values(k - 2)
             if live(k - 3):
                 scale_output(k - 3, slice(0, Y_ON_VECTOR), True)
                 store_output(k - 3)
@@ -435,8 +456,37 @@ def tile_dualstreamattentionwithrotaryembedding_pb_kernel(
                 invert_sums(0)
             if live(k - 1):
                 invert_sums(k - 1)
-                for j in (0, 1, 2, 3):
-                    transpose_e(k - 1, j)
+                if k < ROUNDS - 1:
+                    for j in (0, 1, 2, 3):
+                        transpose_e(k - 1, j)
             if live(k + 2):
                 transpose_qk(k + 2)
                 copy_qk(k + 2)
+
+        a, z = ROUNDS - 2, ROUNDS - 1
+        copy_e(a, 1, nc.vector.tensor_copy)
+        copy_e(a, 0)
+        project_values(a)
+        quantise_values(a - 1)
+        attend(a - 1)
+        for j in range(TILES):
+            transpose_e(z, j)
+        add_bias(a)
+        quantise_e(a)
+        scale_output(a - 1, slice(0, TILES), False)
+        store_output(a - 1)
+        copy_e(z, 0)
+        copy_e(z, 1, nc.vector.tensor_copy)
+        project_values(z)
+        quantise_values(a)
+        attend(a)
+        add_bias(z)
+        invert_sums(z)
+        quantise_e(z)
+        quantise_values(z)
+        scale_output(a, slice(0, TILES), False)
+        store_output(a)
+        attend(z)
+        scale_output(z, slice(2, TILES), False)
+        scale_output(z, slice(0, 2), True)
+        store_output(z)

@@ -23,7 +23,7 @@ TILES = SEQ // P
 PASSES = D // (P * PACK)
 ROUNDS = BATCH * HEADS
 SCALE = 1.0 / math.sqrt(HD)
-Y_ON_VECTOR = 2
+Y_ON_VECTOR = 1
 SCORE_BANKS = 4
 
 FLOPS = 2 * BATCH * SEQ * D * D + 2 * 2 * ROUNDS * SEQ * SEQ * HD
@@ -141,16 +141,9 @@ def tile_dualstreamattentionwithrotaryembedding_pb_kernel(
                 out=tok_codes[b][:].bitcast(FP8X4), scales=tok_scales[b][:], in_=tok_grouped[b][:]
             )
 
-        def spread_bias(h):
-            cols = slice(h * HD, (h + 1) * HD)
-            nc.gpsimd.tensor_scalar(
-                out=bias[:, 1:TILES, cols],
-                in0=bias_x[:, cols].unsqueeze(1).to_broadcast([P, TILES - 1, HD]),
-                scalar1=1.0,
-                scalar2=0.0,
-                op0=ALU.mult,
-                op1=ALU.add,
-            )
+        def spread_bias():
+            for t in range(1, TILES):
+                nc.scalar.copy(out=bias[:, t, :], in_=bias_x[:])
 
         qk_flipped = {}
 
@@ -370,49 +363,53 @@ def tile_dualstreamattentionwithrotaryembedding_pb_kernel(
         for j in range(TILES):
             score_matmul(1, j)
             max_pass(1, j)
+        transpose_qk(2)
+        copy_qk(2)
         exp_tile(1, 0)
         exp_tile(1, 1)
         transpose_tokens(0, 2, ps_et, "e_flipped")
         copy_tokens(0, 2, on_scalar)
         transpose_tokens(0, 3, ps_et, "e_flipped")
         copy_tokens(0, 3, on_vector)
-        transpose_qk(2)
-        copy_qk(2)
         exp_tile(1, 2)
         exp_tile(1, 3)
+        for j in range(TILES):
+            score_matmul(2, j)
+            max_pass(2, j)
         for j in range(TILES):
             transpose_e(0, j)
         copy_e(0, 1)
         copy_e(0, 0)
-        transpose_tokens(1, 0, ps_misc, "misc")
-        copy_tokens(1, 0, on_scalar)
         regroup_weights(0)
         regroup_weights(1)
-        spread_bias(0)
-        spread_bias(1)
         quantise_tokens(0)
+        transpose_tokens(1, 0, ps_misc, "misc")
+        copy_tokens(1, 0, on_scalar)
+        spread_bias()
+        transpose_tokens(1, 1, ps_misc, "misc")
+        copy_tokens(1, 1, on_vector)
         quantise_weights(0)
         quantise_weights(1)
         regroup_weights(2)
         regroup_weights(3)
-        transpose_tokens(1, 1, ps_misc, "misc")
-        copy_tokens(1, 1, on_vector)
-        for j in range(TILES):
-            score_matmul(2, j)
-            max_pass(2, j)
         transpose_qk(3)
         copy_qk(3)
         transpose_tokens(1, 2, ps_et, "e_flipped")
         copy_tokens(1, 2, on_scalar)
         transpose_tokens(1, 3, ps_et, "e_flipped")
         copy_tokens(1, 3, on_vector)
+        quantise_e(0)
+        for j in range(TILES):
+            exp_tile(2, j)
 
         for k in range(2, ROUNDS):
-            if live(k - 2):
-                project_values(k - 2)
-                if k > 2:
-                    copy_e(k - 2, 1)
-                    copy_e(k - 2, 0)
+            project_values(k - 2)
+            if k > 2:
+                copy_e(k - 2, 1)
+                copy_e(k - 2, 0)
+            if live(k + 2):
+                transpose_qk(k + 2)
+                copy_qk(k + 2)
             if k > 2:
                 max_pass(k, 3)
             for j in (0, 1, 2):
@@ -422,52 +419,41 @@ def tile_dualstreamattentionwithrotaryembedding_pb_kernel(
                     score_matmul(k + 1, j)
             if live(k + 1):
                 score_matmul(k + 1, 3)
-            exp_tile(k, 0)
-            exp_tile(k, 3)
+            if k > 2:
+                exp_tile(k, 0)
+                exp_tile(k, 3)
             if k == ROUNDS - 1:
                 exp_tile(k, 2)
                 exp_tile(k, 1)
-                for j in range(TILES):
-                    transpose_e(k - 1, j)
-            if live(k - 2):
-                add_bias(k - 2)
+            add_bias(k - 2)
             if live(k - 3):
-                quantise_values(k - 3)
                 attend(k - 3)
-            if live(k - 2):
+            if k > 2:
                 quantise_e(k - 2)
             if live(k - 3):
                 scale_output(k - 3, slice(Y_ON_VECTOR, TILES), False)
-            if k < ROUNDS - 1:
+            if 2 < k < ROUNDS - 1:
                 exp_tile(k, 2)
                 exp_tile(k, 1)
             if k == 2:
                 quantise_tokens(1)
+            quantise_values(k - 2)
             if live(k - 3):
                 scale_output(k - 3, slice(0, Y_ON_VECTOR), True)
                 store_output(k - 3)
-            if live(k):
-                quantise_weights(k)
-            if live(k + 2):
-                regroup_weights(k + 2)
-                if k % 2 == 0:
-                    spread_bias(k // 2 + 1)
             if k == 2:
                 invert_sums(0)
-            if live(k - 1):
-                invert_sums(k - 1)
-                if k < ROUNDS - 1:
-                    for j in (0, 1, 2, 3):
-                        transpose_e(k - 1, j)
+            invert_sums(k - 1)
+            quantise_weights(k)
             if live(k + 2):
-                transpose_qk(k + 2)
-                copy_qk(k + 2)
+                regroup_weights(k + 2)
+            for j in range(TILES):
+                transpose_e(k - 1, j)
 
         a, z = ROUNDS - 2, ROUNDS - 1
-        copy_e(a, 1, nc.vector.tensor_copy)
-        copy_e(a, 0)
         project_values(a)
-        quantise_values(a - 1)
+        copy_e(a, 1, on_vector)
+        copy_e(a, 0)
         attend(a - 1)
         for j in range(TILES):
             transpose_e(z, j)
@@ -476,7 +462,7 @@ def tile_dualstreamattentionwithrotaryembedding_pb_kernel(
         scale_output(a - 1, slice(0, TILES), False)
         store_output(a - 1)
         copy_e(z, 0)
-        copy_e(z, 1, nc.vector.tensor_copy)
+        copy_e(z, 1, on_vector)
         project_values(z)
         quantise_values(a)
         attend(a)

@@ -309,7 +309,7 @@ def tile_dualstreamattentionwithrotaryembedding_pb_kernel(
 
         def scale_output(r, tiles, on_vector):
             if r not in y_tiles:
-                y_tiles[r] = stage.tile([P, TILES, HD], F32, name="y", bufs=3)
+                y_tiles[r] = stage.tile([P, TILES, HD], F32, name="y", bufs=8)
             y = y_tiles[r]
             inv = inverse[r]
             if tiles.stop == tiles.start:

@@ -232,8 +232,17 @@ def tile_dualstreamattentionwithrotaryembedding_pb_kernel(
             nc.vector.quantize_mx(out=codes[:].bitcast(FP8X4), scales=scales[:], in_=e_grouped[r][:])
             e_words[r] = (codes, scales)
 
-        def regroup_weights(i):
+        def regroup_weights(i, on_vector=False):
             grouped = stage.tile([P, PASSES * HD * PACK], BF16, name="w_grouped", align_bytes=64)
+            w_grouped[i] = grouped
+            if on_vector:
+                nc.vector.tensor_copy(
+                    out=grouped[:].rearrange("p (g c i t) -> p g c t i", g=PASSES, i=4, t=PACK),
+                    in_=w_raw[2 * (i // 4) + i % 2][:, :, :, (i // 2 % 2) * HD : (i // 2 % 2 + 1) * HD].rearrange(
+                        "p g t (c i) -> p g c t i", i=4
+                    ),
+                )
+                return
             nc.gpsimd.tensor_scalar(
                 out=grouped[:].rearrange("p (g n t) -> p g n t", g=PASSES, t=PACK),
                 in0=w_raw[2 * (i // 4) + i % 2][:, :, :, (i // 2 % 2) * HD : (i // 2 % 2 + 1) * HD].rearrange(
@@ -244,7 +253,6 @@ def tile_dualstreamattentionwithrotaryembedding_pb_kernel(
                 op0=ALU.mult,
                 op1=ALU.add,
             )
-            w_grouped[i] = grouped
 
         def quantise_weights(i):
             nc.vector.quantize_mx(
@@ -390,15 +398,15 @@ def tile_dualstreamattentionwithrotaryembedding_pb_kernel(
         copy_tokens(1, 1, on_vector)
         quantise_weights(0)
         quantise_weights(1)
-        regroup_weights(2)
-        regroup_weights(3)
         transpose_qk(3)
         copy_qk(3)
         transpose_tokens(1, 2, ps_et, "e_flipped")
         copy_tokens(1, 2, on_scalar)
         transpose_tokens(1, 3, ps_et, "e_flipped")
         copy_tokens(1, 3, on_vector)
+        regroup_weights(2, True)
         quantise_e(0)
+        regroup_weights(3, True)
         for j in range(TILES):
             exp_tile(2, j)
 
@@ -445,8 +453,8 @@ def tile_dualstreamattentionwithrotaryembedding_pb_kernel(
                 invert_sums(0)
             invert_sums(k - 1)
             quantise_weights(k)
-            if live(k + 2):
-                regroup_weights(k + 2)
+            if k > 2 and live(k + 1):
+                regroup_weights(k + 1)
             for j in range(TILES):
                 transpose_e(k - 1, j)
 

@@ -23,8 +23,8 @@ TILES = SEQ // P
 PASSES = D // (P * PACK)
 ROUNDS = BATCH * HEADS
 SCALE = 1.0 / math.sqrt(HD)
-Y_ON_VECTOR = 1
-SCORE_BANKS = 4
+Y_ON_VECTOR = 2
+SCORE_BANKS = 3
 
 FLOPS = 2 * BATCH * SEQ * D * D + 2 * 2 * ROUNDS * SEQ * SEQ * HD
 
@@ -41,7 +41,7 @@ def tile_dualstreamattentionwithrotaryembedding_pb_kernel(
         small = ctx.enter_context(tc.tile_pool(name="small", bufs=8))
         ps_scores = ctx.enter_context(tc.psum_pool(name="ps_scores", bufs=SCORE_BANKS))
         ps_et = ctx.enter_context(tc.psum_pool(name="ps_et", bufs=2))
-        ps_misc = ctx.enter_context(tc.psum_pool(name="ps_misc", bufs=2))
+        ps_misc = ctx.enter_context(tc.psum_pool(name="ps_misc", bufs=1))
 
         q_raw = []
         k_raw = []
@@ -148,7 +148,7 @@ def tile_dualstreamattentionwithrotaryembedding_pb_kernel(
         qk_flipped = {}
 
         def transpose_qk(r):
-            flipped = ps_misc.tile([P, 2 * SEQ], BF16, name="qk_flipped", tag="misc")
+            flipped = ps_misc.tile([P, 2 * SEQ], BF16, name="qk_flipped", tag="qk")
             for j in range(TILES):
                 nc.tensor.transpose(flipped[:, j * P : (j + 1) * P], q_raw[r][:, j, :], ident_bf[:])
             for j in range(TILES):
@@ -261,7 +261,7 @@ def tile_dualstreamattentionwithrotaryembedding_pb_kernel(
 
         def project_values(r):
             h, b = divmod(r, BATCH)
-            acc = ps_misc.tile([P, TILES, HD], F32, name="v_acc", tag="misc")
+            acc = ps_misc.tile([P, TILES, HD], F32, name="v_acc", tag="v")
             for t in range(TILES):
                 i = 2 * h + (0 if t == 0 else 1)
                 for g in range(PASSES):
@@ -298,7 +298,7 @@ def tile_dualstreamattentionwithrotaryembedding_pb_kernel(
         def attend(r):
             e_codes, e_scales = e_words[r]
             v_codes, v_scales = v_words[r]
-            acc = ps_misc.tile([P, TILES, HD], F32, name="y_acc", tag="misc")
+            acc = ps_misc.tile([P, TILES, HD], F32, name="y_acc", tag="y")
             for j in range(TILES):
                 nc.tensor.matmul_mx(
                     out=acc[:, j, :],
@@ -356,10 +356,11 @@ def tile_dualstreamattentionwithrotaryembedding_pb_kernel(
         score_matmul(0, 1)
         transpose_qk(1)
         score_matmul(0, 2)
+        max_pass(0, 0)
         score_matmul(0, 3)
-        for j in (0, 1):
-            max_pass(0, j)
-            exp_tile(0, j)
+        exp_tile(0, 0)
+        max_pass(0, 1)
+        exp_tile(0, 1)
         copy_qk(1)
         for j in (2, 3):
             max_pass(0, j)
@@ -368,8 +369,11 @@ def tile_dualstreamattentionwithrotaryembedding_pb_kernel(
         copy_tokens(0, 0, on_scalar)
         transpose_tokens(0, 1, ps_et, "e_flipped")
         copy_tokens(0, 1, on_vector)
-        for j in range(TILES):
+        for j in range(3):
             score_matmul(1, j)
+        max_pass(1, 0)
+        score_matmul(1, 3)
+        for j in (1, 2, 3):
             max_pass(1, j)
         transpose_qk(2)
         copy_qk(2)
@@ -381,8 +385,11 @@ def tile_dualstreamattentionwithrotaryembedding_pb_kernel(
         copy_tokens(0, 3, on_vector)
         exp_tile(1, 2)
         exp_tile(1, 3)
-        for j in range(TILES):
+        for j in range(3):
             score_matmul(2, j)
+        max_pass(2, 0)
+        score_matmul(2, 3)
+        for j in (1, 2, 3):
             max_pass(2, j)
         for j in range(TILES):
             transpose_e(0, j)
@@ -391,10 +398,10 @@ def tile_dualstreamattentionwithrotaryembedding_pb_kernel(
         regroup_weights(0)
         regroup_weights(1)
         quantise_tokens(0)
-        transpose_tokens(1, 0, ps_misc, "misc")
+        transpose_tokens(1, 0, ps_misc, "v")
         copy_tokens(1, 0, on_scalar)
         spread_bias()
-        transpose_tokens(1, 1, ps_misc, "misc")
+        transpose_tokens(1, 1, ps_misc, "y")
         copy_tokens(1, 1, on_vector)
         quantise_weights(0)
         quantise_weights(1)
@@ -409,77 +416,84 @@ def tile_dualstreamattentionwithrotaryembedding_pb_kernel(
         regroup_weights(3, True)
         for j in range(TILES):
             exp_tile(2, j)
+        project_values(0)
+        for j in range(3):
+            score_matmul(3, j)
+        add_bias(0)
+        quantise_tokens(1)
+        quantise_values(0)
+        for r in range(2):
+            invert_sums(r)
+        quantise_weights(2)
+        quantise_weights(3)
+        regroup_weights(4)
+        for j in range(TILES):
+            transpose_e(1, j)
+        copy_e(1, 1)
+        copy_e(1, 0)
+        transpose_qk(4)
+        copy_qk(4)
+        project_values(1)
 
-        for k in range(2, ROUNDS):
-            project_values(k - 2)
-            if k > 2:
-                copy_e(k - 2, 1)
-                copy_e(k - 2, 0)
+        for k in range(3, ROUNDS):
+            attend(k - 3)
+            max_pass(k, 0)
+            score_matmul(k, 3)
+            exp_tile(k, 0)
+            max_pass(k, 1)
+            if live(k + 1):
+                score_matmul(k + 1, 0)
+            exp_tile(k, 1)
+            scale_output(k - 3, slice(Y_ON_VECTOR, TILES), False)
+            max_pass(k, 2)
+            if live(k + 1):
+                score_matmul(k + 1, 1)
             if live(k + 2):
                 transpose_qk(k + 2)
-                copy_qk(k + 2)
-            if k > 2:
-                max_pass(k, 3)
-            for j in (0, 1, 2):
-                if k > 2:
-                    max_pass(k, j)
-                if live(k + 1):
-                    score_matmul(k + 1, j)
+            max_pass(k, 3)
             if live(k + 1):
-                score_matmul(k + 1, 3)
-            if k > 2:
-                exp_tile(k, 0)
-                exp_tile(k, 3)
-            if k == ROUNDS - 1:
-                exp_tile(k, 2)
-                exp_tile(k, 1)
+                score_matmul(k + 1, 2)
+            exp_tile(k, 3)
+            exp_tile(k, 2)
+            if live(k + 2):
+                copy_qk(k + 2)
             add_bias(k - 2)
-            if live(k - 3):
-                attend(k - 3)
-            if k > 2:
-                quantise_e(k - 2)
-            if live(k - 3):
-                scale_output(k - 3, slice(Y_ON_VECTOR, TILES), False)
-            if 2 < k < ROUNDS - 1:
-                exp_tile(k, 2)
-                exp_tile(k, 1)
-            if k == 2:
-                quantise_tokens(1)
+            scale_output(k - 3, slice(0, Y_ON_VECTOR), True)
+            store_output(k - 3)
+            quantise_e(k - 2)
             quantise_values(k - 2)
-            if live(k - 3):
-                scale_output(k - 3, slice(0, Y_ON_VECTOR), True)
-                store_output(k - 3)
-            if k == 2:
-                invert_sums(0)
             invert_sums(k - 1)
-            quantise_weights(k)
-            if k > 2 and live(k + 1):
-                regroup_weights(k + 1)
+            if live(k + 1):
+                quantise_weights(k + 1)
+            if live(k + 2):
+                regroup_weights(k + 2)
             for j in range(TILES):
                 transpose_e(k - 1, j)
+            copy_e(k - 1, 1, on_vector if k == ROUNDS - 1 else on_scalar)
+            copy_e(k - 1, 0)
+            if k < ROUNDS - 1:
+                project_values(k - 1)
 
         a, z = ROUNDS - 2, ROUNDS - 1
         project_values(a)
-        copy_e(a, 1, on_vector)
-        copy_e(a, 0)
-        attend(a - 1)
         for j in range(TILES):
             transpose_e(z, j)
-        add_bias(a)
         quantise_e(a)
-        scale_output(a - 1, slice(0, TILES), False)
-        store_output(a - 1)
+        add_bias(a)
         copy_e(z, 0)
         copy_e(z, 1, on_vector)
+        attend(a - 1)
         project_values(z)
+        scale_output(a - 1, slice(0, TILES), False)
+        store_output(a - 1)
         quantise_values(a)
         attend(a)
-        add_bias(z)
         invert_sums(z)
         quantise_e(z)
-        quantise_values(z)
+        add_bias(z)
         scale_output(a, slice(0, TILES), False)
         store_output(a)
+        quantise_values(z)
         attend(z)
         scale_output(z, slice(2, TILES), False)
         scale_output(z, slice(0, 2), True)

from contextlib import ExitStack
import math

import concourse.mybir as mybir
from concourse.masks import make_identity

F32 = mybir.dt.float32
BF16 = mybir.dt.bfloat16
U32 = mybir.dt.uint32
U8 = mybir.dt.uint8
FP8X4 = mybir.dt.float8_e4m3fn_x4
ALU = mybir.AluOpType
ACT = mybir.ActivationFunctionType

P = 128
PACK = 4
BATCH = 2
HEADS = 8
HD = 128
D = HEADS * HD
SEQ = 512
TILES = SEQ // P
PASSES = D // (P * PACK)
ROUNDS = BATCH * HEADS
SCALE = 1.0 / math.sqrt(HD)
Y_ON_VECTOR = 2
SCORE_BANKS = 3

FLOPS = 2 * BATCH * SEQ * D * D + 2 * 2 * ROUNDS * SEQ * SEQ * HD


def tile_dualstreamattentionwithrotaryembedding_pb_kernel(
    tc, q_rot, k_rot, x, c, Wv_x, bv_x, Wv_c, bv_c, out_0, out_1
):
    nc = tc.nc
    with ExitStack() as ctx:
        const = ctx.enter_context(tc.tile_pool(name="const", bufs=1))
        raw = ctx.enter_context(tc.tile_pool(name="raw", bufs=1))
        keep = ctx.enter_context(tc.tile_pool(name="keep", bufs=1))
        stage = ctx.enter_context(tc.tile_pool(name="stage", bufs=2))
        small = ctx.enter_context(tc.tile_pool(name="small", bufs=8))
        ps_scores = ctx.enter_context(tc.psum_pool(name="ps_scores", bufs=SCORE_BANKS))
        ps_et = ctx.enter_context(tc.psum_pool(name="ps_et", bufs=2))
        ps_misc = ctx.enter_context(tc.psum_pool(name="ps_misc", bufs=1))

        q_raw = []
        k_raw = []
        for r in range(ROUNDS):
            q_raw.append(raw.tile([P, TILES, HD], BF16, name="q_raw%d" % r))
            k_raw.append(raw.tile([P, TILES, HD], BF16, name="k_raw%d" % r))
        tok_raw = [raw.tile([P, TILES, D], BF16, name="tok_raw%d" % b) for b in range(BATCH)]
        w_raw = [raw.tile([P, PASSES, PACK, 2 * HD], BF16, name="w_raw%d" % i) for i in range(HEADS)]
        bias_x = const.tile([P, D], BF16)
        bias = const.tile([P, TILES, D], BF16)

        def load_qk(r):
            h, b = divmod(r, BATCH)
            nc.sync.dma_start(out=q_raw[r][:], in_=q_rot[b, h].rearrange("(j p) d -> p j d", p=P))
            nc.sync.dma_start(out=k_raw[r][:], in_=k_rot[b, h].rearrange("(j p) d -> p j d", p=P))

        def load_tokens(b):
            nc.sync.dma_start(out=tok_raw[b][:, 0, :], in_=c[b])
            nc.sync.dma_start(
                out=tok_raw[b][:, 1:TILES, :], in_=x[b].rearrange("(j p) k -> p j k", p=P)
            )

        def load_weights(pair):
            for w, weights in enumerate((Wv_c, Wv_x)):
                rows = weights.rearrange("(a p e) n -> p a e n", p=P, e=2)
                slots = w_raw[2 * pair + w][:].rearrange("p g (u e) n -> p (g u) e n", e=2)
                cols = slice(2 * pair * HD, 2 * (pair + 1) * HD)
                for e in range(2):
                    nc.sync.dma_start(out=slots[:, :, e, :], in_=rows[:, :, e, cols])

        load_qk(0)
        load_qk(1)
        load_tokens(0)
        load_qk(2)
        load_weights(0)
        load_qk(3)
        load_tokens(1)
        nc.sync.dma_start(out=bias[:, 0, :], in_=bv_c.partition_broadcast(P))
        nc.sync.dma_start(out=bias_x[:], in_=bv_x.partition_broadcast(P))
        for r in range(4, ROUNDS):
            load_qk(r)
            if r % 4 == 0:
                load_weights(r // 4)

        ident_bf = const.tile([P, P], BF16)
        make_identity(nc, ident_bf[:])
        ident_f32 = const.tile([P, P], F32)
        make_identity(nc, ident_f32[:])

        warm = const.tile([P, 1], F32)
        nc.vector.memset(warm[:], 0.0)
        nc.scalar.activation(out=warm[:], in_=warm[:], func=ACT.Exp)

        tok_codes = [keep.tile([P, TILES * PASSES * P], U32, name="tok_codes%d" % b, align_bytes=64) for b in range(BATCH)]
        tok_scales = [keep.tile([P, TILES * PASSES * P], U8, name="tok_scales%d" % b, align_bytes=64) for b in range(BATCH)]
        w_codes = [keep.tile([P, PASSES * HD], U32, name="w_codes%d" % i, align_bytes=64) for i in range(2 * HEADS)]
        w_scales = [keep.tile([P, PASSES * HD], U8, name="w_scales%d" % i, align_bytes=64) for i in range(2 * HEADS)]

        tok_flipped = {}
        tok_grouped = {}
        qk_t = {}
        s_tiles = {}
        e_flipped = {}
        u_tiles = {}
        e_tiles = {}
        w_grouped = {}
        e_grouped = {}
        e_words = {}
        v_grouped = {}
        inverse = {}
        v_words = {}
        v_acc = {}
        y_acc = {}
        y_tiles = {}
        row_sums = {}

        def transpose_tokens(b, t, pool, tag):
            words = tok_raw[b][:, t, :].bitcast(F32)
            flipped = pool.tile([P, PASSES * 2, P], F32, name="tok_flipped", tag=tag)
            for a in range(PASSES * 2):
                nc.tensor.transpose(flipped[:, a, :], words[:, a * P : (a + 1) * P], ident_f32[:])
            tok_flipped[(b, t)] = flipped

        def copy_tokens(b, t, copy):
            if b not in tok_grouped:
                tok_grouped[b] = stage.tile([P, TILES * PASSES * P * PACK], BF16, name="tok_grouped", align_bytes=64)
            span = PASSES * P * PACK
            copy(
                out=tok_grouped[b][:, t * span : (t + 1) * span]
                .bitcast(F32)
                .rearrange("p (g m u) -> p g m u", g=PASSES, u=2),
                in_=tok_flipped[(b, t)][:].rearrange("p (g u) m -> p g m u", u=2),
            )

        def quantise_tokens(b):
            nc.vector.quantize_mx(
                out=tok_codes[b][:].bitcast(FP8X4), scales=tok_scales[b][:], in_=tok_grouped[b][:]
            )

        def spread_bias():
            for t in range(1, TILES):
                nc.scalar.copy(out=bias[:, t, :], in_=bias_x[:])

        qk_flipped = {}

        def transpose_qk(r):
            flipped = ps_misc.tile([P, 2 * SEQ], BF16, name="qk_flipped", tag="qk")
            for j in range(TILES):
                nc.tensor.transpose(flipped[:, j * P : (j + 1) * P], q_raw[r][:, j, :], ident_bf[:])
            for j in range(TILES):
                nc.tensor.transpose(
                    flipped[:, SEQ + j * P : SEQ + (j + 1) * P], k_raw[r][:, j, :], ident_bf[:]
                )
            qk_flipped[r] = flipped

        def copy_qk(r):
            qk_t[r] = stage.tile([P, 2 * SEQ], BF16, name="qk_t", bufs=3)
            if r == 0:
                nc.vector.tensor_copy(out=qk_t[r][:, :SEQ], in_=qk_flipped[r][:, :SEQ])
                nc.scalar.copy(out=qk_t[r][:, SEQ:], in_=qk_flipped[r][:, SEQ:])
            else:
                nc.scalar.copy(out=qk_t[r][:], in_=qk_flipped[r][:])

        def score_matmul(r, j):
            scores = ps_scores.tile([P, SEQ], F32, name="scores")
            nc.tensor.matmul(
                out=scores[:],
                lhsT=qk_t[r][:, j * P : (j + 1) * P],
                rhs=qk_t[r][:, SEQ : 2 * SEQ],
                start=True,
                stop=True,
            )
            s_tiles[(r, j)] = scores

        def max_pass(r, j):
            scores = s_tiles[(r, j)]
            u = stage.tile([P, SEQ], F32, name="u", bufs=12)
            shift = small.tile([P, 1], F32, name="shift")
            nc.vector.tensor_scalar(
                out=u[:].rearrange("p (v m w) -> p v m w", v=2, w=2),
                in0=scores[:].rearrange("p (v w m) -> p v m w", v=2, w=2),
                scalar1=-SCALE,
                scalar2=None,
                op0=ALU.mult,
                op1=ALU.min,
                accum_out=shift[:],
            )
            u_tiles[(r, j)] = (u, shift)

        def exp_tile(r, j):
            if r not in row_sums:
                row_sums[r] = small.tile([P, TILES], F32, name="row_sums")
            u, shift = u_tiles[(r, j)]
            e = stage.tile([P, SEQ], BF16, name="e", bufs=8)
            nc.scalar.activation(
                out=e[:],
                in_=u[:],
                func=ACT.Exp,
                bias=shift[:],
                scale=-1.0,
                accum_out=row_sums[r][:, j : j + 1],
            )
            e_tiles[(r, j)] = e

        def transpose_e(r, j):
            if (r, j // 2) not in e_flipped:
                e_flipped[(r, j // 2)] = ps_et.tile([P, 2, TILES // 2, P], F32, name="e_flipped")
            words = e_tiles[(r, j)][:].bitcast(F32)
            for v in range(TILES // 2):
                nc.tensor.transpose(
                    e_flipped[(r, j // 2)][:, j % 2, v, :], words[:, v * P : (v + 1) * P], ident_f32[:]
                )

        def copy_e(r, pair, copy=nc.scalar.copy):
            if r not in e_grouped:
                e_grouped[r] = stage.tile([P, SEQ * PACK], BF16, name="e_grouped", align_bytes=64)
            span = 2 * P * PACK
            copy(
                out=e_grouped[r][:, pair * span : (pair + 1) * span]
                .bitcast(F32)
                .rearrange("p (a m v) -> p a m v", a=2, v=TILES // 2),
                in_=e_flipped[(r, pair)][:].rearrange("p a v m -> p a m v"),
            )

        def quantise_e(r):
            codes = stage.tile([P, SEQ], U32, name="e_codes", align_bytes=64, bufs=4)
            scales = stage.tile([P, SEQ], U8, name="e_scales", align_bytes=64, bufs=4)
            nc.vector.quantize_mx(out=codes[:].bitcast(FP8X4), scales=scales[:], in_=e_grouped[r][:])
            e_words[r] = (codes, scales)

        def regroup_weights(i, on_vector=False):
            grouped = stage.tile([P, PASSES * HD * PACK], BF16, name="w_grouped", align_bytes=64)
            w_grouped[i] = grouped
            if on_vector:
                nc.vector.tensor_copy(
                    out=grouped[:].rearrange("p (g c i t) -> p g c t i", g=PASSES, i=4, t=PACK),
                    in_=w_raw[2 * (i // 4) + i % 2][:, :, :, (i // 2 % 2) * HD : (i // 2 % 2 + 1) * HD].rearrange(
                        "p g t (c i) -> p g c t i", i=4
                    ),
                )
                return
            nc.gpsimd.tensor_scalar(
                out=grouped[:].rearrange("p (g n t) -> p g n t", g=PASSES, t=PACK),
                in0=w_raw[2 * (i // 4) + i % 2][:, :, :, (i // 2 % 2) * HD : (i // 2 % 2 + 1) * HD].rearrange(
                    "p g t n -> p g n t"
                ),
                scalar1=1.0,
                scalar2=0.0,
                op0=ALU.mult,
                op1=ALU.add,
            )

        def quantise_weights(i):
            nc.vector.quantize_mx(
                out=w_codes[i][:].bitcast(FP8X4), scales=w_scales[i][:], in_=w_grouped[i][:]
            )

        def project_values(r):
            h, b = divmod(r, BATCH)
            acc = ps_misc.tile([P, TILES, HD], F32, name="v_acc", tag="v")
            for t in range(TILES):
                i = 2 * h + (0 if t == 0 else 1)
                for g in range(PASSES):
                    tok = slice((t * PASSES + g) * P, (t * PASSES + g + 1) * P)
                    col = slice(g * HD, (g + 1) * HD)
                    nc.tensor.matmul_mx(
                        out=acc[:, t, :],
                        lhsT=tok_codes[b][:, tok].bitcast(FP8X4),
                        lhsT_scale=tok_scales[b][:, tok],
                        rhs=w_codes[i][:, col].bitcast(FP8X4),
                        rhs_scale=w_scales[i][:, col],
                        start=(g == 0),
                        stop=(g == PASSES - 1),
                    )
            v_acc[r] = acc

        def add_bias(r):
            h = r // BATCH
            grouped = stage.tile([P, HD * PACK], BF16, name="v_grouped", align_bytes=64, bufs=3)
            nc.vector.tensor_tensor(
                out=grouped[:].rearrange("p (n t) -> p n t", t=PACK),
                in0=v_acc[r][:].rearrange("p t n -> p n t"),
                in1=bias[:, :, h * HD : (h + 1) * HD].rearrange("p t n -> p n t"),
                op=ALU.add,
            )
            v_grouped[r] = grouped

        def quantise_values(r):
            codes = stage.tile([P, HD], U32, name="v_codes", align_bytes=64, bufs=3)
            scales = stage.tile([P, HD], U8, name="v_scales", align_bytes=64, bufs=3)
            nc.vector.quantize_mx(out=codes[:].bitcast(FP8X4), scales=scales[:], in_=v_grouped[r][:])
            v_words[r] = (codes, scales)

        def attend(r):
            e_codes, e_scales = e_words[r]
            v_codes, v_scales = v_words[r]
            acc = ps_misc.tile([P, TILES, HD], F32, name="y_acc", tag="y")
            for j in range(TILES):
                nc.tensor.matmul_mx(
                    out=acc[:, j, :],
                    lhsT=e_codes[:, j * P : (j + 1) * P].bitcast(FP8X4),
                    lhsT_scale=e_scales[:, j * P : (j + 1) * P],
                    rhs=v_codes[:].bitcast(FP8X4),
                    rhs_scale=v_scales[:],
                    start=True,
                    stop=True,
                )
            y_acc[r] = acc

        def invert_sums(r):
            inverse[r] = small.tile([P, TILES], F32, name="inverse")
            nc.vector.reciprocal(out=inverse[r][:], in_=row_sums[r][:])

        def scale_output(r, tiles, on_vector):
            if r not in y_tiles:
                y_tiles[r] = stage.tile([P, TILES, HD], F32, name="y", bufs=8)
            y = y_tiles[r]
            inv = inverse[r]
            if tiles.stop == tiles.start:
                pass
            elif on_vector:
                nc.vector.tensor_tensor(
                    out=y[:, tiles, :],
                    in0=y_acc[r][:, tiles, :],
                    in1=inv[:, tiles].unsqueeze(2).to_broadcast([P, tiles.stop - tiles.start, HD]),
                    op=ALU.mult,
                )
            else:
                for j in reversed(range(tiles.start, tiles.stop)):
                    nc.scalar.activation(
                        out=y[:, j, :], in_=y_acc[r][:, j, :], func=ACT.Copy, scale=inv[:, j : j + 1]
                    )

        def store_output(r):
            h, b = divmod(r, BATCH)
            y = y_tiles[r]
            cols = slice(h * HD, (h + 1) * HD)
            nc.sync.dma_start(out=out_1[b, :, cols], in_=y[:, 0, :])
            nc.sync.dma_start(
                out=out_0[b].rearrange("(j p) d -> p j d", p=P)[:, :, cols], in_=y[:, 1:TILES, :]
            )

        def live(r):
            return 0 <= r < ROUNDS

        ctx.enter_context(tc.manual_schedule())
        on_scalar, on_vector = nc.scalar.copy, nc.vector.tensor_copy

        transpose_qk(0)
        copy_qk(0)
        score_matmul(0, 0)
        score_matmul(0, 1)
        transpose_qk(1)
        score_matmul(0, 2)
        max_pass(0, 0)
        score_matmul(0, 3)
        exp_tile(0, 0)
        max_pass(0, 1)
        exp_tile(0, 1)
        copy_qk(1)
        for j in (2, 3):
            max_pass(0, j)
            exp_tile(0, j)
        transpose_tokens(0, 0, ps_et, "e_flipped")
        copy_tokens(0, 0, on_scalar)
        transpose_tokens(0, 1, ps_et, "e_flipped")
        copy_tokens(0, 1, on_vector)
        for j in range(3):
            score_matmul(1, j)
        max_pass(1, 0)
        score_matmul(1, 3)
        for j in (1, 2, 3):
            max_pass(1, j)
        transpose_qk(2)
        copy_qk(2)
        exp_tile(1, 0)
        exp_tile(1, 1)
        transpose_tokens(0, 2, ps_et, "e_flipped")
        copy_tokens(0, 2, on_scalar)
        transpose_tokens(0, 3, ps_et, "e_flipped")
        copy_tokens(0, 3, on_vector)
        exp_tile(1, 2)
        exp_tile(1, 3)
        for j in range(3):
            score_matmul(2, j)
        max_pass(2, 0)
        score_matmul(2, 3)
        for j in (1, 2, 3):
            max_pass(2, j)
        for j in range(TILES):
            transpose_e(0, j)
        copy_e(0, 1)
        copy_e(0, 0)
        regroup_weights(0)
        regroup_weights(1)
        quantise_tokens(0)
        transpose_tokens(1, 0, ps_misc, "v")
        copy_tokens(1, 0, on_scalar)
        spread_bias()
        transpose_tokens(1, 1, ps_misc, "y")
        copy_tokens(1, 1, on_vector)
        quantise_weights(0)
        quantise_weights(1)
        transpose_qk(3)
        copy_qk(3)
        transpose_tokens(1, 2, ps_et, "e_flipped")
        copy_tokens(1, 2, on_scalar)
        transpose_tokens(1, 3, ps_et, "e_flipped")
        copy_tokens(1, 3, on_vector)
        regroup_weights(2, True)
        quantise_e(0)
        regroup_weights(3, True)
        for j in range(TILES):
            exp_tile(2, j)
        project_values(0)
        for j in range(3):
            score_matmul(3, j)
        add_bias(0)
        quantise_tokens(1)
        quantise_values(0)
        for r in range(2):
            invert_sums(r)
        quantise_weights(2)
        quantise_weights(3)
        regroup_weights(4)
        for j in range(TILES):
            transpose_e(1, j)
        copy_e(1, 1)
        copy_e(1, 0)
        transpose_qk(4)
        copy_qk(4)
        project_values(1)

        for k in range(3, ROUNDS):
            attend(k - 3)
            max_pass(k, 0)
            score_matmul(k, 3)
            exp_tile(k, 0)
            max_pass(k, 1)
            if live(k + 1):
                score_matmul(k + 1, 0)
            exp_tile(k, 1)
            scale_output(k - 3, slice(Y_ON_VECTOR, TILES), False)
            max_pass(k, 2)
            if live(k + 1):
                score_matmul(k + 1, 1)
            if live(k + 2):
                transpose_qk(k + 2)
            max_pass(k, 3)
            if live(k + 1):
                score_matmul(k + 1, 2)
            exp_tile(k, 3)
            exp_tile(k, 2)
            if live(k + 2):
                copy_qk(k + 2)
            add_bias(k - 2)
            scale_output(k - 3, slice(0, Y_ON_VECTOR), True)
            store_output(k - 3)
            quantise_e(k - 2)
            quantise_values(k - 2)
            invert_sums(k - 1)
            if live(k + 1):
                quantise_weights(k + 1)
            if live(k + 2):
                regroup_weights(k + 2)
            for j in range(TILES):
                transpose_e(k - 1, j)
            copy_e(k - 1, 1, on_vector if k == ROUNDS - 1 else on_scalar)
            copy_e(k - 1, 0)
            if k < ROUNDS - 1:
                project_values(k - 1)

        a, z = ROUNDS - 2, ROUNDS - 1
        project_values(a)
        for j in range(TILES):
            transpose_e(z, j)
        quantise_e(a)
        add_bias(a)
        copy_e(z, 0)
        copy_e(z, 1, on_vector)
        attend(a - 1)
        project_values(z)
        scale_output(a - 1, slice(0, TILES), False)
        store_output(a - 1)
        quantise_values(a)
        attend(a)
        invert_sums(z)
        quantise_e(z)
        add_bias(z)
        scale_output(a, slice(0, TILES), False)
        store_output(a)
        quantise_values(z)
        attend(z)
        scale_output(z, slice(2, TILES), False)
        scale_output(z, slice(0, 2), True)
        store_output(z)
